import numpy as np
import ml_dtypes


def mxq(x, axis, fmt="e4m3"):
    dtype, down = {"e4m3": (ml_dtypes.float8_e4m3fn, 7), "e5m2": (ml_dtypes.float8_e5m2, 14)}[fmt]
    v = np.moveaxis(np.asarray(x, np.float32).astype(ml_dtypes.bfloat16).astype(np.float64), axis, -1)
    blocks = v.reshape(v.shape[:-1] + (-1, 32))
    amax = np.abs(blocks).max(-1, keepdims=True)
    byte = np.maximum(np.where(amax > 0, np.frexp(amax)[1] - 1 + 127, 0) - down, 1)
    scale = np.exp2(byte - 127.0)
    codes = (blocks / scale).astype(np.float32).astype(dtype).astype(np.float64)
    return np.moveaxis((codes * scale).reshape(v.shape), -1, axis)


WIDE = False


def mx_kscale(k):
    if not WIDE:
        return np.ones(k)
    levels = np.array([10, -10, 5, -5, 0])
    if k % 512:
        return np.exp2(np.random.permutation(np.resize(levels, k // 32))).repeat(32)
    a = np.empty((k // 512, 16))
    for p in range(k // 512):
        a[p, :8] = np.random.permutation(np.resize(levels, 8))
        for g in range(8):
            far = levels[np.abs(levels - a[p, g]) >= 10]
            a[p, g + 8] = far[np.random.randint(len(far))]
    return np.exp2(a.ravel()).repeat(32)


BF16 = ml_dtypes.bfloat16


def bf(x):
    return np.asarray(x, np.float32).astype(BF16)


def f64(x):
    return np.asarray(x).astype(np.float64)


B, N, HID, ITERS = 512, 32, 2048, 10
DOUT = N * N
SLOPE = 0.01
EPS = 1e-8


def leaky(v):
    return np.where(v >= 0.0, v, SLOPE * v)


def l1_normalize(r, axis):
    return r / np.maximum(np.abs(r).sum(axis=axis, keepdims=True), EPS)


def setup_inputs():
    s, t = mx_kscale(HID), mx_kscale(HID)
    return {"h3": bf(leaky(np.random.standard_normal((B, HID)) * 1.1) * s),
            "W4": bf(np.random.standard_normal((HID, HID)) * 1.4 / np.sqrt(HID) / s[:, None] * t),
            "b4": bf(np.random.standard_normal(HID) * 0.3 * t),
            "W5": bf(np.random.standard_normal((HID, DOUT)) * 2.0 / np.sqrt(HID) / t[:, None]),
            "b5": bf(np.random.standard_normal(DOUT) * 3.0 - 4.0)}


def reference(h3, W4, b4, W5, b5):
    h4 = leaky((mxq(f64(h3), 1, "e4m3") @ mxq(f64(W4), 0, "e4m3")) + f64(b4))
    r = ((mxq(h4, 1, "e4m3") @ mxq(f64(W5), 0, "e4m3")) + f64(b5)).reshape(B, N, N)
    r = np.logaddexp(r, 0.0)
    for _ in range(ITERS):
        r = l1_normalize(r, 1)
        r = l1_normalize(r, 2)
    return r

@@ -1,0 +1,401 @@
+from contextlib import ExitStack
+
+import concourse.mybir as mybir
+from concourse.masks import make_identity
+
+F32 = mybir.dt.float32
+BF16 = mybir.dt.bfloat16
+U32 = mybir.dt.uint32
+U8 = mybir.dt.uint8
+FP8X4 = mybir.dt.float8_e4m3fn_x4
+ALU = mybir.AluOpType
+ACT = mybir.ActivationFunctionType
+AXIS = mybir.AxisListType
+
+P = 128
+PACK = 4
+K_PASS = P * PACK
+BATCH, SIDE, HID, ROUNDS = 512, 32, 2048, 10
+DOUT = SIDE * SIDE
+SLOPE = 0.01
+EPS = 1e-8
+PASSES = HID // K_PASS
+BATCH_TILES = BATCH // P
+BANK = 512
+BANKS = 8
+W_CHUNK = 1024
+CHUNK_TILES = W_CHUNK // P
+AHEAD = 3
+GROUPED_BUFS = 3
+ACTS_BUFS = 2
+RUN = 4
+VECTOR_COLS = 448
+I_LO = P // SIDE
+D_TILES = DOUT // P
+HALVES = DOUT // BANK
+PER_HALF = BANK // P
+LINEAR_FROM = 30.0
+OWN_TILES = 2
+VECTOR_SUMS = 24
+TINY = 1e-24
+
+FLOPS = 2 * BATCH * HID * (HID + DOUT)
+
+
+def tile_matchingnet_pa_kernel(tc, h3, W4, b4, W5, b5, out):
+    nc = tc.nc
+    with ExitStack() as whole:
+        consts = whole.enter_context(tc.tile_pool(name="consts", bufs=1))
+        banks = whole.enter_context(tc.psum_pool(name="banks", bufs=BANKS))
+
+        tiny = consts.tile([P, 1], F32, name="tiny")
+        nc.vector.memset(tiny[:], TINY)
+        warm = consts.tile([P, 1], F32, name="warm")
+        nc.scalar.activation(out=warm[:], in_=tiny[:], func=ACT.Exp)
+
+        ident = consts.tile([P, P], F32, name="ident")
+        make_identity(nc, ident[:])
+        swap = consts.tile([P, P], F32, name="swap")
+        nc.vector.tensor_copy(
+            out=swap[:].rearrange("p (j i) -> p j i", i=I_LO),
+            in_=ident[:].rearrange("p (i j) -> p j i", i=I_LO),
+        )
+
+        with ExitStack() as front:
+            keep = front.enter_context(tc.tile_pool(name="keep", bufs=1))
+            wraw = front.enter_context(tc.tile_pool(name="wraw", bufs=AHEAD + 1))
+            stage = front.enter_context(tc.tile_pool(name="stage", bufs=GROUPED_BUFS))
+            acts = front.enter_context(tc.tile_pool(name="acts", bufs=ACTS_BUFS))
+
+            chunks = [("w4", block, g) for block in range(HID // W_CHUNK) for g in range(PASSES)]
+            chunks += [("w5", 0, g) for g in range(PASSES)]
+            raws = {}
+
+            def load(n):
+                weights, block, g = chunks[n]
+                raw = wraw.tile([P, PACK, W_CHUNK], BF16, name="raw")
+                cols = slice(W_CHUNK * block, W_CHUNK * (block + 1))
+                rows = (W4 if weights == "w4" else W5)[K_PASS * g : K_PASS * (g + 1), cols]
+                nc.sync.dma_start(out=raw[:], in_=rows.rearrange("(p t) w -> p t w", t=PACK))
+                raws[n] = raw
+
+            h3_rows = [keep.tile([P, HID], BF16, name="h3_rows%d" % bt) for bt in range(BATCH_TILES)]
+            for bt in range(BATCH_TILES):
+                nc.sync.dma_start(out=h3_rows[bt][:], in_=h3[bt * P : (bt + 1) * P, :])
+                if bt == BATCH_TILES // 2 - 1:
+                    load(0)
+            for n in range(1, AHEAD):
+                load(n)
+
+            h3_grouped = [
+                keep.tile([P, BATCH * PACK], BF16, align_bytes=64, name="h3_grouped%d" % g) for g in range(PASSES)
+            ]
+            h3_codes = keep.tile([P, PASSES, BATCH], U32, align_bytes=64, name="h3_codes")
+            h3_scales = keep.tile([P, PASSES, BATCH], U8, align_bytes=64, name="h3_scales")
+            for pair in range(BATCH_TILES // 2):
+                for g in range(PASSES):
+                    flipped = banks.tile([P, 2, 2, P], F32, tag="bank", name="flipped")
+                    for member in range(2):
+                        words = h3_rows[2 * pair + member][:].bitcast(F32)
+                        for u in range(2):
+                            first = (K_PASS // 2) * g
+                            nc.tensor.transpose(
+                                flipped[:, member, u, :], words[:, first + u : first + K_PASS // 2 : 2], ident[:]
+                            )
+                    dst = (
+                        h3_grouped[g][:]
+                        .bitcast(F32)
+                        .rearrange("p (b u) -> p b u", u=2)[:, 2 * P * pair : 2 * P * (pair + 1), :]
+                        .rearrange("p (y b) u -> p y b u", y=2)
+                    )
+                    src = flipped[:].rearrange("p y u b -> p y b u")
+                    if g % 2 == 0:
+                        nc.vector.tensor_copy(out=dst, in_=src)
+                    else:
+                        nc.scalar.copy(out=dst, in_=src)
+            for g in range(PASSES):
+                nc.vector.quantize_mx(
+                    out=h3_codes[:, g, :].bitcast(FP8X4), scales=h3_scales[:, g, :], in_=h3_grouped[g][:]
+                )
+
+            b4_rows = HID // P
+            bias_cols = consts.tile([P, b4_rows + D_TILES], F32, name="bias_cols")
+            b4_cols = consts.tile([P, PASSES, PACK], BF16, name="b4_cols")
+            with nc.allow_non_contiguous_dma("runs of four biases"):
+                nc.sync.dma_start(out=b4_cols[:], in_=b4.rearrange("(g p t) -> p g t", p=P, t=PACK))
+            nc.vector.tensor_copy(
+                out=bias_cols[:, 0:b4_rows].rearrange("p (g t) -> p g t", t=PACK), in_=b4_cols[:]
+            )
+            bias_rows = consts.tile([P, P], BF16, name="bias_rows")
+            nc.vector.memset(bias_rows[:], 0.0)
+            nc.sync.dma_start(out=bias_rows[0:D_TILES, :], in_=b5.rearrange("(row col) -> row col", col=P))
+            bias_rows_f32 = consts.tile([P, P], F32, name="bias_rows_f32")
+            nc.vector.tensor_copy(out=bias_rows_f32[:], in_=bias_rows[:])
+            bias_bank = banks.tile([P, P], F32, tag="bank", name="bias_bank")
+            nc.tensor.transpose(bias_bank[:], bias_rows_f32[:], ident[:])
+            nc.vector.tensor_copy(out=bias_cols[:, b4_rows : b4_rows + D_TILES], in_=bias_bank[:, 0:D_TILES])
+
+            w_codes = {
+                "w4": keep.tile([P, PASSES, HID], U32, align_bytes=64, name="w4_codes"),
+                "w5": keep.tile([P, PASSES, DOUT], U32, align_bytes=64, name="w5_codes"),
+            }
+            w_scales = {
+                "w4": keep.tile([P, PASSES, HID], U8, align_bytes=64, name="w4_scales"),
+                "w5": keep.tile([P, PASSES, DOUT], U8, align_bytes=64, name="w5_scales"),
+            }
+            h4_codes = keep.tile([P, PASSES, BATCH], U32, align_bytes=64, name="h4_codes")
+            h4_scales = keep.tile([P, PASSES, BATCH], U8, align_bytes=64, name="h4_scales")
+            moving = {"w4": (h3_codes, h3_scales), "w5": (h4_codes, h4_scales)}
+            groupeds = {}
+
+            def regroup(n):
+                grouped = stage.tile([P, W_CHUNK, PACK], BF16, align_bytes=64, name="grouped")
+                if chunks[n][0] == "w5":
+                    src = raws[n][:].rearrange("p t (w r) -> p w t r", r=RUN)
+                    dst = grouped[:].rearrange("p (w r) t -> p w t r", r=RUN)
+                    cut = VECTOR_COLS // RUN
+                    nc.vector.tensor_copy(out=dst[:, :cut], in_=src[:, :cut])
+                    nc.scalar.copy(out=dst[:, cut:], in_=src[:, cut:])
+                else:
+                    for half in range(W_CHUNK // K_PASS):
+                        cols = slice(K_PASS * half, K_PASS * (half + 1))
+                        src = raws[n][:, :, cols].rearrange("p t (m s) -> p s m t", s=PACK)
+                        dst = grouped[:, cols, :].rearrange("p (s m) t -> p s m t", s=PACK)
+                        if half == 0:
+                            whole_tiles, rest = divmod(VECTOR_COLS, P)
+                            nc.vector.tensor_copy(out=dst[:, :whole_tiles], in_=src[:, :whole_tiles])
+                            nc.vector.tensor_copy(out=dst[:, whole_tiles, :rest], in_=src[:, whole_tiles, :rest])
+                            nc.scalar.copy(out=dst[:, whole_tiles, rest:], in_=src[:, whole_tiles, rest:])
+                        else:
+                            nc.scalar.copy(out=dst, in_=src)
+                groupeds[n] = grouped
+
+            def quantise_and_multiply(n, sums_banks):
+                weights, block, g = chunks[n]
+                cols = slice(W_CHUNK * block, W_CHUNK * (block + 1))
+                nc.vector.quantize_mx(
+                    out=w_codes[weights][:, g, cols].bitcast(FP8X4),
+                    scales=w_scales[weights][:, g, cols],
+                    in_=groupeds[n][:].rearrange("p w t -> p (w t)"),
+                )
+                for m in range(CHUNK_TILES):
+                    first = W_CHUNK * block + P * m
+                    nc.tensor.matmul_mx(
+                        out=sums_banks[m][:],
+                        lhsT=w_codes[weights][:, g, first : first + P].bitcast(FP8X4),
+                        lhsT_scale=w_scales[weights][:, g, first : first + P],
+                        rhs=moving[weights][0][:, g, :].bitcast(FP8X4),
+                        rhs_scale=moving[weights][1][:, g, :],
+                        start=(g == 0),
+                        stop=(g == PASSES - 1),
+                    )
+
+            def activate(block, sums_banks):
+                for quad in range(CHUNK_TILES // PACK):
+                    g2 = (CHUNK_TILES // PACK) * block + quad
+                    biased = acts.tile([P, PACK, BATCH], F32, name="biased")
+                    for t in range(PACK):
+                        m = PACK * g2 + t
+                        nc.scalar.activation(
+                            out=biased[:, t, :],
+                            in_=sums_banks[PACK * quad + t][:],
+                            func=ACT.Identity,
+                            bias=bias_cols[:, m : m + 1],
+                            scale=1.0,
+                        )
+                    h4_grouped = acts.tile([P, BATCH, PACK], BF16, align_bytes=64, name="h4_grouped")
+                    by_column = biased[:].rearrange("p t b -> p b t")
+                    nc.vector.scalar_tensor_tensor(
+                        out=h4_grouped[:], in0=by_column, scalar=SLOPE, in1=by_column, op0=ALU.mult, op1=ALU.max
+                    )
+                    nc.vector.quantize_mx(
+                        out=h4_codes[:, g2, :].bitcast(FP8X4),
+                        scales=h4_scales[:, g2, :],
+                        in_=h4_grouped[:].rearrange("p b t -> p (b t)"),
+                    )
+
+            sums_banks = []
+            for n in range(len(chunks) + 1):
+                if n + AHEAD < len(chunks):
+                    load(n + AHEAD)
+                if n < len(chunks):
+                    regroup(n)
+                if n > 0:
+                    weights, block, g = chunks[n - 1]
+                    if g == 0:
+                        sums_banks = [
+                            banks.tile([P, BANK], F32, tag="bank", name="sums_bank%d" % m) for m in range(CHUNK_TILES)
+                        ]
+                    quantise_and_multiply(n - 1, sums_banks)
+                    if weights == "w4" and g == PASSES - 1:
+                        activate(block, sums_banks)
+            z_banks = sums_banks
+
+        with ExitStack() as back:
+            soft = back.enter_context(tc.tile_pool(name="soft", bufs=1))
+
+            expo = soft.tile([P, D_TILES, BATCH], F32, name="expo")
+            r_flipped = soft.tile([P, D_TILES, BATCH], F32, name="r_flipped")
+            for d in range(D_TILES):
+                b5_col = bias_cols[:, b4_rows + d : b4_rows + d + 1]
+                nc.vector.tensor_scalar(
+                    out=expo[:, d, :], in0=z_banks[d][:], scalar1=b5_col, scalar2=LINEAR_FROM, op0=ALU.add, op1=ALU.min
+                )
+                nc.scalar.activation(out=expo[:, d, :], in_=expo[:, d, :], func=ACT.Exp)
+
+            own_tiles = range(OWN_TILES)
+            lent_tiles = range(OWN_TILES, BATCH_TILES)
+            orders = {"col": swap, "row": ident}
+            matrices = {"col": {}, "row": {}}
+
+            def flip_back(label, bt, h):
+                bank = banks.tile([P, BANK], F32, tag="bank", name="r_bank")
+                for part in range(PER_HALF):
+                    nc.tensor.transpose(
+                        bank[:, P * part : P * (part + 1)],
+                        r_flipped[:, PER_HALF * h + part, P * bt : P * (bt + 1)],
+                        orders[label][:],
+                    )
+                return bank
+
+            for label in ("col", "row"):
+                for bt in lent_tiles:
+                    matrices[label][bt] = [soft.tile([P, DOUT], F32, name="r_%s_%d" % (label, bt))]
+            staged = []
+            for h in range(HALVES):
+                for part in range(PER_HALF):
+                    d = PER_HALF * h + part
+                    b5_col = bias_cols[:, b4_rows + d : b4_rows + d + 1]
+                    nc.scalar.activation(out=expo[:, d, :], in_=expo[:, d, :], func=ACT.Ln, bias=1.0, scale=1.0)
+                    nc.vector.scalar_tensor_tensor(
+                        out=r_flipped[:, d, :], in0=z_banks[d][:], scalar=b5_col, in1=expo[:, d, :], op0=ALU.add, op1=ALU.max
+                    )
+                for label in ("col", "row"):
+                    for bt in lent_tiles:
+                        staged.append((label, bt, h, flip_back(label, bt, h)))
+            for label, bt, h, bank in staged:
+                in_sbuf = matrices[label][bt][0][:, BANK * h : BANK * (h + 1)]
+                if label == "col":
+                    nc.vector.tensor_copy(out=in_sbuf, in_=bank[:])
+                else:
+                    nc.scalar.copy(out=in_sbuf, in_=bank[:])
+            for bt in own_tiles:
+                for label in ("col", "row"):
+                    matrices[label][bt] = [flip_back(label, bt, h) for h in range(HALVES)]
+            nc.scalar.activation(out=warm[:], in_=tiny[:], func=ACT.Abs_reciprocal_sqrt)
+
+            state = []
+            for bt in range(BATCH_TILES):
+                vectors = {}
+                for name in ("a", "c"):
+                    vectors[name] = soft.tile([P, SIDE], F32, name="%s%d" % (name, bt))
+                    vectors["bounds_" + name] = soft.tile([P, 2, SIDE], F32, name="bounds_%s%d" % (name, bt))
+                    nc.vector.memset(vectors["bounds_" + name][:, 1, :], EPS)
+                vectors["divisor"] = soft.tile([P, SIDE], F32, name="divisor%d" % bt)
+                vectors["root"] = soft.tile([P, SIDE], F32, name="root%d" % bt)
+                vectors["prod"] = soft.tile([P, DOUT], F32, name="prod%d" % bt)
+                state.append(vectors)
+            for bt in own_tiles:
+                nc.vector.memset(state[bt]["a"][:], 1.0)
+            unused = {bt: soft.tile([P, SIDE - VECTOR_SUMS, SIDE], F32, name="unused%d" % bt) for bt in lent_tiles}
+
+            def factor_of(step):
+                return "c" if step % 2 == 0 else "a"
+
+            def multiply(bt, step):
+                engine = nc.vector if bt in own_tiles else nc.gpsimd
+                vectors = state[bt]
+                pieces = matrices["col" if step % 2 == 0 else "row"][bt]
+                width = DOUT // len(pieces)
+                span = width // SIDE
+                for h, piece in enumerate(pieces):
+                    target = vectors["prod"][:, width * h : width * (h + 1)]
+                    if step % 2 == 0:
+                        a_here = vectors["a"][:, span * h : span * (h + 1)].rearrange("p (d i) -> p d i", i=I_LO)
+                        engine.tensor_tensor(
+                            out=target.rearrange("p (d j i) -> p d j i", j=SIDE, i=I_LO),
+                            in0=piece[:].rearrange("p (d j i) -> p d j i", j=SIDE, i=I_LO),
+                            in1=a_here.unsqueeze(2).to_broadcast([P, span // I_LO, SIDE, I_LO]),
+                            op=ALU.mult,
+                        )
+                    else:
+                        engine.tensor_tensor(
+                            out=target.rearrange("p (i j) -> p i j", j=SIDE),
+                            in0=piece[:].rearrange("p (i j) -> p i j", j=SIDE),
+                            in1=vectors["c"][:].unsqueeze(1).to_broadcast([P, span, SIDE]),
+                            op=ALU.mult,
+                        )
+
+            def terms_of(bt, step):
+                if step == 0 and bt in lent_tiles:
+                    terms = matrices["col"][bt][0][:]
+                else:
+                    terms = state[bt]["prod"][:]
+                if step % 2 == 0:
+                    return terms.rearrange("p (d j i) -> p j d i", j=SIDE, i=I_LO)
+                return terms.rearrange("p (i j) -> p i j", j=SIDE)
+
+            def add_up_on_vector(bt, step, count):
+                sums = state[bt]["bounds_" + factor_of(step)][:, 0, :]
+                nc.vector.tensor_reduce(
+                    out=sums[:, :count],
+                    in_=terms_of(bt, step)[:, :count],
+                    axis=AXIS.XY if step % 2 == 0 else AXIS.X,
+                    op=ALU.add,
+                )
+
+            def add_up_on_scalar(bt, step, done):
+                sums = state[bt]["bounds_" + factor_of(step)][:, 0, :]
+                terms = terms_of(bt, step)
+                for s in range(done, SIDE):
+                    copied = unused[bt][:, s - done, :]
+                    if step % 2 == 0:
+                        copied = copied.rearrange("p (d i) -> p d i", i=I_LO)
+                    nc.scalar.activation(out=copied, in_=terms[:, s], func=ACT.Copy, accum_out=sums[:, s : s + 1])
+
+            def renew(bt, step):
+                vectors = state[bt]
+                factor = factor_of(step)
+                bounds = vectors["bounds_" + factor]
+                nc.vector.tensor_reduce(
+                    out=vectors["divisor"][:], in_=bounds[:].rearrange("p plane s -> p s plane"), axis=AXIS.X, op=ALU.max
+                )
+                nc.scalar.activation(
+                    out=vectors["root"][:], in_=vectors["divisor"][:], func=ACT.Abs_reciprocal_sqrt, bias=tiny[:], scale=1.0
+                )
+                nc.scalar.activation(out=vectors[factor][:], in_=vectors["root"][:], func=ACT.Square)
+                nc.scalar.mul(out=bounds[:, 1, :], in_=vectors["divisor"][:], mul=EPS)
+
+            def finish(bt, engine):
+                vectors = state[bt]
+                by_matrix = vectors["prod"][:].rearrange("p (i j) -> p i j", j=SIDE)
+                engine.tensor_tensor(
+                    out=by_matrix,
+                    in0=by_matrix,
+                    in1=vectors["a"][:].unsqueeze(2).to_broadcast([P, SIDE, SIDE]),
+                    op=ALU.mult,
+                )
+                nc.sync.dma_start(out=out[P * bt : P * (bt + 1)].rearrange("b i j -> b (i j)"), in_=vectors["prod"][:])
+
+            steps = 2 * ROUNDS
+            pairs = [(bt, bt + OWN_TILES) for bt in own_tiles]
+            with tc.manual_schedule():
+                waiting = None
+                for step in range(steps):
+                    for own, lent in pairs:
+                        add_up_on_scalar(lent, step, VECTOR_SUMS)
+                        multiply(own, step)
+                        if waiting is not None:
+                            renew(waiting[0], waiting[1])
+                        add_up_on_vector(lent, step, VECTOR_SUMS)
+                        add_up_on_vector(own, step, SIDE)
+                        renew(lent, step)
+                        if step + 1 < steps:
+                            multiply(lent, step + 1)
+                        elif lent != pairs[-1][1]:
+                            finish(lent, nc.gpsimd)
+                        waiting = (own, step)
+                renew(waiting[0], waiting[1])
+                finish(pairs[0][0], nc.vector)
+                finish(pairs[-1][1], nc.vector)
+                finish(pairs[-1][0], nc.vector)

@@ -16,6 +16,7 @@ P = 128
 PACK = 4
 K_PASS = P * PACK
 BATCH, SIDE, HID, ROUNDS = 512, 32, 2048, 10
+STEPS = 2 * ROUNDS
 DOUT = SIDE * SIDE
 SLOPE = 0.01
 EPS = 1e-8
@@ -35,8 +36,19 @@ D_TILES = DOUT // P
 HALVES = DOUT // BANK
 PER_HALF = BANK // P
 LINEAR_FROM = 30.0
-OWN_TILES = 2
-VECTOR_SUMS = 24
+HALF_SIDE = SIDE // HALVES
+BLOCK_TILE, OWN_TILES, LENT_TILE = 0, (1, 2), 3
+QUADS = P // SIDE
+LANES = P // SIDE
+BLOCKS = SIDE // LANES
+UNIT = QUADS * LANES
+GROUPS = 2
+GROUP_BLOCKS = BLOCKS // GROUPS
+GROUP_COLS = GROUP_BLOCKS * UNIT
+REPEATS = 6
+VECTOR_SUMS = 8
+QUARTERS = 4
+QUARTER_SUMS = SIDE // QUARTERS
 TINY = 1e-24
 
 FLOPS = 2 * BATCH * HID * (HID + DOUT)
@@ -55,11 +67,17 @@ def tile_matchingnet_pa_kernel(tc, h3, W4, b4, W5, b5, out):
 
         ident = consts.tile([P, P], F32, name="ident")
         make_identity(nc, ident[:])
-        swap = consts.tile([P, P], F32, name="swap")
-        nc.vector.tensor_copy(
-            out=swap[:].rearrange("p (j i) -> p j i", i=I_LO),
-            in_=ident[:].rearrange("p (i j) -> p j i", i=I_LO),
-        )
+        lane_mask = consts.tile([P, LANES], F32, name="lane_mask")
+        quad_mask = consts.tile([P, QUADS], F32, name="quad_mask")
+        pick_i = consts.tile([P, SIDE], F32, name="pick_i")
+        pick_j = consts.tile([P, SIDE], F32, name="pick_j")
+        for column_sums, view in (
+            (lane_mask, ident[:].rearrange("p (i x) -> p x i", x=LANES)),
+            (quad_mask, ident[:].rearrange("p (y j) -> p y j", y=QUADS)),
+            (pick_i, ident[:].rearrange("p (i x) -> p i x", x=LANES)),
+            (pick_j, ident[:].rearrange("p (y j) -> p j y", y=QUADS)),
+        ):
+            nc.vector.tensor_reduce(out=column_sums[:], in_=view, axis=AXIS.X, op=ALU.add)
 
         with ExitStack() as front:
             keep = front.enter_context(tc.tile_pool(name="keep", bufs=1))
@@ -242,160 +260,253 @@ def tile_matchingnet_pa_kernel(tc, h3, W4, b4, W5, b5, out):
                     out=expo[:, d, :], in0=z_banks[d][:], scalar1=b5_col, scalar2=LINEAR_FROM, op0=ALU.add, op1=ALU.min
                 )
                 nc.scalar.activation(out=expo[:, d, :], in_=expo[:, d, :], func=ACT.Exp)
+            for d in range(D_TILES):
+                b5_col = bias_cols[:, b4_rows + d : b4_rows + d + 1]
+                nc.scalar.activation(out=expo[:, d, :], in_=expo[:, d, :], func=ACT.Ln, bias=1.0, scale=1.0)
+                nc.vector.scalar_tensor_tensor(
+                    out=r_flipped[:, d, :], in0=z_banks[d][:], scalar=b5_col, in1=expo[:, d, :], op0=ALU.add, op1=ALU.max
+                )
 
-            own_tiles = range(OWN_TILES)
-            lent_tiles = range(OWN_TILES, BATCH_TILES)
-            orders = {"col": swap, "row": ident}
-            matrices = {"col": {}, "row": {}}
-
-            def flip_back(label, bt, h):
+            def flip_back(bt, h):
                 bank = banks.tile([P, BANK], F32, tag="bank", name="r_bank")
                 for part in range(PER_HALF):
                     nc.tensor.transpose(
                         bank[:, P * part : P * (part + 1)],
                         r_flipped[:, PER_HALF * h + part, P * bt : P * (bt + 1)],
-                        orders[label][:],
+                        ident[:],
                     )
                 return bank
 
-            for label in ("col", "row"):
-                for bt in lent_tiles:
-                    matrices[label][bt] = [soft.tile([P, DOUT], F32, name="r_%s_%d" % (label, bt))]
-            staged = []
+            squares = soft.tile([P, DOUT], F32, align_bytes=64, name="squares")
+            by_j = soft.tile([P, DOUT], F32, name="by_j")
+            by_i = soft.tile([P, DOUT], F32, name="by_i")
+            block_banks = [flip_back(BLOCK_TILE, h) for h in range(HALVES)]
             for h in range(HALVES):
-                for part in range(PER_HALF):
-                    d = PER_HALF * h + part
-                    b5_col = bias_cols[:, b4_rows + d : b4_rows + d + 1]
-                    nc.scalar.activation(out=expo[:, d, :], in_=expo[:, d, :], func=ACT.Ln, bias=1.0, scale=1.0)
-                    nc.vector.scalar_tensor_tensor(
-                        out=r_flipped[:, d, :], in0=z_banks[d][:], scalar=b5_col, in1=expo[:, d, :], op0=ALU.add, op1=ALU.max
-                    )
-                for label in ("col", "row"):
-                    for bt in lent_tiles:
-                        staged.append((label, bt, h, flip_back(label, bt, h)))
-            for label, bt, h, bank in staged:
-                in_sbuf = matrices[label][bt][0][:, BANK * h : BANK * (h + 1)]
-                if label == "col":
-                    nc.vector.tensor_copy(out=in_sbuf, in_=bank[:])
+                nc.vector.transpose(squares[:, BANK * h : BANK * (h + 1)], block_banks[h][:])
+                nc.scalar.copy(
+                    out=by_j[:].rearrange("p (T i x) -> p T i x", T=BLOCKS, x=LANES)[
+                        :, :, HALF_SIDE * h : HALF_SIDE * (h + 1), :
+                    ],
+                    in_=squares[:, BANK * h : BANK * (h + 1)].rearrange("p (i T x) -> p T i x", T=BLOCKS, x=LANES),
+                )
+            lent_ij = soft.tile([P, DOUT], F32, name="lent_ij")
+            lent_ji = soft.tile([P, DOUT], F32, name="lent_ji")
+            for h in range(HALVES):
+                bank = flip_back(LENT_TILE, h)
+                nc.vector.tensor_copy(
+                    out=lent_ji[:].rearrange("p (j i) -> p j i", i=SIDE)[:, :, HALF_SIDE * h : HALF_SIDE * (h + 1)],
+                    in_=bank[:].rearrange("p (i j) -> p j i", j=SIDE),
+                )
+                nc.scalar.copy(out=lent_ij[:, BANK * h : BANK * (h + 1)], in_=bank[:])
+            own_banks = {bt: [flip_back(bt, h) for h in range(HALVES)] for bt in OWN_TILES}
+            per_bank = BANK // P
+            for part in range(BLOCKS // per_bank):
+                bank = banks.tile([P, BANK], F32, tag="bank", name="turned")
+                for q in range(per_bank):
+                    block = per_bank * part + q
+                    nc.tensor.transpose(bank[:, P * q : P * (q + 1)], by_j[:, P * block : P * (block + 1)], ident[:])
+                turned = by_i[:, BANK * part : BANK * (part + 1)]
+                if part == 0:
+                    nc.vector.tensor_copy(out=turned, in_=bank[:])
                 else:
-                    nc.scalar.copy(out=in_sbuf, in_=bank[:])
-            for bt in own_tiles:
-                for label in ("col", "row"):
-                    matrices[label][bt] = [flip_back(label, bt, h) for h in range(HALVES)]
+                    nc.scalar.copy(out=turned, in_=bank[:])
             nc.scalar.activation(out=warm[:], in_=tiny[:], func=ACT.Abs_reciprocal_sqrt)
 
-            state = []
-            for bt in range(BATCH_TILES):
-                vectors = {}
-                for name in ("a", "c"):
-                    vectors[name] = soft.tile([P, SIDE], F32, name="%s%d" % (name, bt))
-                    vectors["bounds_" + name] = soft.tile([P, 2, SIDE], F32, name="bounds_%s%d" % (name, bt))
-                    nc.vector.memset(vectors["bounds_" + name][:, 1, :], EPS)
-                vectors["divisor"] = soft.tile([P, SIDE], F32, name="divisor%d" % bt)
-                vectors["root"] = soft.tile([P, SIDE], F32, name="root%d" % bt)
-                vectors["prod"] = soft.tile([P, DOUT], F32, name="prod%d" % bt)
-                state.append(vectors)
-            for bt in own_tiles:
+            names = ("c", "a")
+
+            keep_only = {"c": quad_mask, "a": lane_mask}
+            groups = []
+            for g in range(GROUPS):
+                parts = {}
+                for name in names:
+                    for kind in ("", "divisor_", "root_"):
+                        parts[kind + name] = soft.tile([P, GROUP_COLS], F32, name="%s%s_g%d" % (kind, name, g))
+                    nc.gpsimd.memset(parts["divisor_" + name][:], 1.0)
+                nc.vector.tensor_copy(
+                    out=parts["a"][:].rearrange("p (T x y) -> p T x y", x=LANES, y=QUADS),
+                    in_=lane_mask[:].unsqueeze(1).unsqueeze(3).to_broadcast([P, GROUP_BLOCKS, LANES, QUADS]),
+                )
+                parts["sums"] = banks.tile([P, BANK], F32, tag="bank", name="sums_g%d" % g)
+                groups.append(parts)
+            natural = {name: soft.tile([P, P], F32, name="natural_%s" % name) for name in names}
+
+            def add_up_blocks(g, step):
+                parts = groups[g]
+                blocks, factor = (by_i, parts["a"]) if step % 2 == 0 else (by_j, parts["c"])
+                for T in range(GROUP_BLOCKS):
+                    block = GROUP_BLOCKS * g + T
+                    cols = slice(UNIT * T, UNIT * (T + 1))
+                    columns = factor[:, cols].rearrange("p (u v) -> p v u", u=LANES)
+                    nc.tensor.matmul(
+                        parts["sums"][:, 0 : REPEATS * GROUP_COLS].rearrange("p (r c) -> p r c", r=REPEATS)[:, :, cols],
+                        blocks[:, P * block : P * (block + 1)],
+                        columns.unsqueeze(1).to_broadcast([P, REPEATS, QUADS, LANES]),
+                        start=True,
+                        stop=True,
+                    )
+
+            def place(g, name, target):
+                root = groups[g]["root_" + name][:].rearrange("p (T u v) -> p u T v", u=LANES, v=QUADS)
+                for u in range(LANES):
+                    nc.scalar.activation(
+                        out=target[:, u], in_=root[:, u], func=ACT.Square, scale=keep_only[name][:, u : u + 1]
+                    )
+
+            def renew_blocks(g, step):
+                parts = groups[g]
+                name = names[step % 2]
+                divisor, root = parts["divisor_" + name], parts["root_" + name]
+                nc.vector.scalar_tensor_tensor(
+                    out=divisor[:], in0=divisor[:], scalar=EPS, in1=parts["sums"][:, 0:GROUP_COLS], op0=ALU.mult, op1=ALU.max
+                )
+                nc.scalar.activation(out=root[:], in_=divisor[:], func=ACT.Abs_reciprocal_sqrt, bias=tiny[:], scale=1.0)
+                if step + 1 < STEPS:
+                    place(g, name, parts[name][:].rearrange("p (T u v) -> p u T v", u=LANES, v=QUADS))
+                if step + 2 >= STEPS:
+                    pattern = "p (u T v) -> p u T v" if name == "c" else "p (v T u) -> p u T v"
+                    columns = natural[name][:].rearrange(pattern, T=BLOCKS, u=LANES)
+                    place(g, name, columns[:, :, GROUP_BLOCKS * g : GROUP_BLOCKS * (g + 1), :])
+
+            def to_rows(name):
+                rows = soft.tile([P, SIDE], F32, name="rows_%s" % name)
+                first = REPEATS * GROUP_COLS + (0 if name == "c" else 2 * SIDE)
+                bank = groups[0]["sums"][:, first : first + SIDE]
+                nc.tensor.matmul(bank, natural[name][:], (pick_j if name == "c" else pick_i)[:], start=True, stop=True)
+                nc.scalar.copy(out=rows[:], in_=bank)
+                return rows
+
+            state = {}
+            for bt in OWN_TILES + (LENT_TILE,):
+                mine = {}
+                for name in names:
+                    mine[name] = soft.tile([P, SIDE], F32, name="%s%d" % (name, bt))
+                    mine["bounds_" + name] = soft.tile([P, 2, SIDE], F32, name="bounds_%s%d" % (name, bt))
+                    nc.vector.memset(mine["bounds_" + name][:, 1, :], EPS)
+                mine["divisor"] = soft.tile([P, SIDE], F32, name="divisor%d" % bt)
+                mine["root"] = soft.tile([P, SIDE], F32, name="root%d" % bt)
+                mine["prod"] = soft.tile([P, DOUT], F32, name="prod%d" % bt)
+                state[bt] = mine
+            for bt in OWN_TILES:
                 nc.vector.memset(state[bt]["a"][:], 1.0)
-            unused = {bt: soft.tile([P, SIDE - VECTOR_SUMS, SIDE], F32, name="unused%d" % bt) for bt in lent_tiles}
+            unused = soft.tile([P, SIDE, SIDE], F32, name="unused")
 
-            def factor_of(step):
-                return "c" if step % 2 == 0 else "a"
-
-            def multiply(bt, step):
-                engine = nc.vector if bt in own_tiles else nc.gpsimd
-                vectors = state[bt]
-                pieces = matrices["col" if step % 2 == 0 else "row"][bt]
-                width = DOUT // len(pieces)
-                span = width // SIDE
-                for h, piece in enumerate(pieces):
-                    target = vectors["prod"][:, width * h : width * (h + 1)]
+            def multiply_own(bt, step):
+                mine = state[bt]
+                for h, bank in enumerate(own_banks[bt]):
+                    rows = slice(HALF_SIDE * h, HALF_SIDE * (h + 1))
                     if step % 2 == 0:
-                        a_here = vectors["a"][:, span * h : span * (h + 1)].rearrange("p (d i) -> p d i", i=I_LO)
-                        engine.tensor_tensor(
-                            out=target.rearrange("p (d j i) -> p d j i", j=SIDE, i=I_LO),
-                            in0=piece[:].rearrange("p (d j i) -> p d j i", j=SIDE, i=I_LO),
-                            in1=a_here.unsqueeze(2).to_broadcast([P, span // I_LO, SIDE, I_LO]),
-                            op=ALU.mult,
-                        )
+                        out_view = mine["prod"][:].rearrange("p (j i) -> p j i", i=SIDE)[:, :, rows]
+                        in_view = bank[:].rearrange("p (i j) -> p j i", j=SIDE)
+                        factor = mine["a"][:, rows].unsqueeze(1).to_broadcast([P, SIDE, HALF_SIDE])
                     else:
-                        engine.tensor_tensor(
-                            out=target.rearrange("p (i j) -> p i j", j=SIDE),
-                            in0=piece[:].rearrange("p (i j) -> p i j", j=SIDE),
-                            in1=vectors["c"][:].unsqueeze(1).to_broadcast([P, span, SIDE]),
-                            op=ALU.mult,
-                        )
+                        out_view = mine["prod"][:].rearrange("p (i j) -> p i j", j=SIDE)[:, rows, :]
+                        in_view = bank[:].rearrange("p (i j) -> p i j", j=SIDE)
+                        factor = mine["c"][:].unsqueeze(1).to_broadcast([P, HALF_SIDE, SIDE])
+                    nc.vector.tensor_tensor(out=out_view, in0=in_view, in1=factor, op=ALU.mult)
 
-            def terms_of(bt, step):
-                if step == 0 and bt in lent_tiles:
-                    terms = matrices["col"][bt][0][:]
-                else:
-                    terms = state[bt]["prod"][:]
-                if step % 2 == 0:
-                    return terms.rearrange("p (d j i) -> p j d i", j=SIDE, i=I_LO)
-                return terms.rearrange("p (i j) -> p i j", j=SIDE)
-
-            def add_up_on_vector(bt, step, count):
-                sums = state[bt]["bounds_" + factor_of(step)][:, 0, :]
+            def add_up_own(bt, step):
+                mine = state[bt]
                 nc.vector.tensor_reduce(
-                    out=sums[:, :count],
-                    in_=terms_of(bt, step)[:, :count],
-                    axis=AXIS.XY if step % 2 == 0 else AXIS.X,
+                    out=mine["bounds_" + names[step % 2]][:, 0, :],
+                    in_=mine["prod"][:].rearrange("p (s t) -> p s t", t=SIDE),
+                    axis=AXIS.X,
                     op=ALU.add,
                 )
 
-            def add_up_on_scalar(bt, step, done):
-                sums = state[bt]["bounds_" + factor_of(step)][:, 0, :]
-                terms = terms_of(bt, step)
-                for s in range(done, SIDE):
-                    copied = unused[bt][:, s - done, :]
-                    if step % 2 == 0:
-                        copied = copied.rearrange("p (d i) -> p d i", i=I_LO)
-                    nc.scalar.activation(out=copied, in_=terms[:, s], func=ACT.Copy, accum_out=sums[:, s : s + 1])
+            def multiply_lent(step):
+                mine = state[LENT_TILE]
+                matrix, factor = (lent_ji, mine["a"]) if step % 2 == 0 else (lent_ij, mine["c"])
+                for quarter in range(QUARTERS):
+                    rows = slice(QUARTER_SUMS * quarter, QUARTER_SUMS * (quarter + 1))
+                    nc.gpsimd.tensor_tensor(
+                        out=mine["prod"][:].rearrange("p (s t) -> p s t", t=SIDE)[:, rows, :],
+                        in0=matrix[:].rearrange("p (s t) -> p s t", t=SIDE)[:, rows, :],
+                        in1=factor[:].unsqueeze(1).to_broadcast([P, QUARTER_SUMS, SIDE]),
+                        op=ALU.mult,
+                    )
+
+            def add_up_lent(step, quarter):
+                mine = state[LENT_TILE]
+                terms = (lent_ji if step == 0 else mine["prod"])[:].rearrange("p (s t) -> p s t", t=SIDE)
+                if quarter == 0:
+                    nc.vector.tensor_reduce(
+                        out=mine["bounds_" + names[step % 2]][:, 0, :VECTOR_SUMS],
+                        in_=terms[:, :VECTOR_SUMS, :],
+                        axis=AXIS.X,
+                        op=ALU.add,
+                    )
+                for s in range(max(VECTOR_SUMS, QUARTER_SUMS * quarter), QUARTER_SUMS * (quarter + 1)):
+                    nc.scalar.activation(
+                        out=unused[:, s, :],
+                        in_=terms[:, s, :],
+                        func=ACT.Copy,
+                        accum_out=mine["bounds_" + names[step % 2]][:, 0, s : s + 1],
+                    )
 
             def renew(bt, step):
-                vectors = state[bt]
-                factor = factor_of(step)
-                bounds = vectors["bounds_" + factor]
+                mine = state[bt]
+                name = names[step % 2]
+                bounds = mine["bounds_" + name]
                 nc.vector.tensor_reduce(
-                    out=vectors["divisor"][:], in_=bounds[:].rearrange("p plane s -> p s plane"), axis=AXIS.X, op=ALU.max
+                    out=mine["divisor"][:], in_=bounds[:].rearrange("p plane s -> p s plane"), axis=AXIS.X, op=ALU.max
                 )
                 nc.scalar.activation(
-                    out=vectors["root"][:], in_=vectors["divisor"][:], func=ACT.Abs_reciprocal_sqrt, bias=tiny[:], scale=1.0
+                    out=mine["root"][:], in_=mine["divisor"][:], func=ACT.Abs_reciprocal_sqrt, bias=tiny[:], scale=1.0
                 )
-                nc.scalar.activation(out=vectors[factor][:], in_=vectors["root"][:], func=ACT.Square)
-                nc.scalar.mul(out=bounds[:, 1, :], in_=vectors["divisor"][:], mul=EPS)
+                nc.scalar.activation(out=mine[name][:], in_=mine["root"][:], func=ACT.Square)
+                nc.scalar.mul(out=bounds[:, 1, :], in_=mine["divisor"][:], mul=EPS)
 
-            def finish(bt, engine):
-                vectors = state[bt]
-                by_matrix = vectors["prod"][:].rearrange("p (i j) -> p i j", j=SIDE)
-                engine.tensor_tensor(
-                    out=by_matrix,
-                    in0=by_matrix,
-                    in1=vectors["a"][:].unsqueeze(2).to_broadcast([P, SIDE, SIDE]),
-                    op=ALU.mult,
+            def store(bt, result):
+                nc.sync.dma_start(out=out[P * bt : P * (bt + 1)].rearrange("b i j -> b (i j)"), in_=result[:])
+
+            def finish(bt, result, a):
+                by_matrix = result[:].rearrange("p (i j) -> p i j", j=SIDE)
+                nc.vector.tensor_tensor(
+                    out=by_matrix, in0=by_matrix, in1=a[:].unsqueeze(2).to_broadcast([P, SIDE, SIDE]), op=ALU.mult
                 )
-                nc.sync.dma_start(out=out[P * bt : P * (bt + 1)].rearrange("b i j -> b (i j)"), in_=vectors["prod"][:])
+                store(bt, result)
 
-            steps = 2 * ROUNDS
-            pairs = [(bt, bt + OWN_TILES) for bt in own_tiles]
+            def finish_lent():
+                mine = state[LENT_TILE]
+                for i in range(SIDE):
+                    row = slice(SIDE * i, SIDE * (i + 1))
+                    nc.scalar.activation(
+                        out=mine["prod"][:, row], in_=mine["prod"][:, row], func=ACT.Copy, scale=mine["a"][:, i : i + 1]
+                    )
+                store(LENT_TILE, mine["prod"])
+
+            first_own, second_own = OWN_TILES
+            block_result = soft.tile([P, DOUT], F32, name="block_result")
             with tc.manual_schedule():
-                waiting = None
-                for step in range(steps):
-                    for own, lent in pairs:
-                        add_up_on_scalar(lent, step, VECTOR_SUMS)
-                        multiply(own, step)
-                        if waiting is not None:
-                            renew(waiting[0], waiting[1])
-                        add_up_on_vector(lent, step, VECTOR_SUMS)
-                        add_up_on_vector(own, step, SIDE)
-                        renew(lent, step)
-                        if step + 1 < steps:
-                            multiply(lent, step + 1)
-                        elif lent != pairs[-1][1]:
-                            finish(lent, nc.gpsimd)
-                        waiting = (own, step)
-                renew(waiting[0], waiting[1])
-                finish(pairs[0][0], nc.vector)
-                finish(pairs[-1][1], nc.vector)
-                finish(pairs[-1][0], nc.vector)
+                for step in range(STEPS):
+                    for g in range(GROUPS):
+                        add_up_blocks(g, step)
+                    multiply_own(first_own, step)
+                    if step > 0:
+                        renew(LENT_TILE, step - 1)
+                        multiply_lent(step)
+                    renew_blocks(0, step)
+                    add_up_own(first_own, step)
+                    add_up_lent(step, 0)
+                    add_up_lent(step, 1)
+                    renew(first_own, step)
+                    multiply_own(second_own, step)
+                    add_up_lent(step, 2)
+                    renew_blocks(1, step)
+                    add_up_lent(step, 3)
+                    add_up_own(second_own, step)
+                    renew(second_own, step)
+                renew(LENT_TILE, STEPS - 1)
+                rows_c = to_rows("c")
+                rows_a = to_rows("a")
+                finish_lent()
+                for h in range(HALVES):
+                    nc.vector.tensor_tensor(
+                        out=block_result[:, BANK * h : BANK * (h + 1)].rearrange("p (i j) -> p i j", j=SIDE),
+                        in0=block_banks[h][:].rearrange("p (i j) -> p i j", j=SIDE),
+                        in1=rows_c[:].unsqueeze(1).to_broadcast([P, HALF_SIDE, SIDE]),
+                        op=ALU.mult,
+                    )
+                for bt in OWN_TILES:
+                    finish(bt, state[bt]["prod"], state[bt]["a"])
+                finish(BLOCK_TILE, block_result, rows_a)

@@ -37,18 +37,18 @@ HALVES = DOUT // BANK
 PER_HALF = BANK // P
 LINEAR_FROM = 30.0
 HALF_SIDE = SIDE // HALVES
-BLOCK_TILE, OWN_TILES, LENT_TILE = 0, (1, 2), 3
+BLOCK_TILES, OWN_TILE, LENT_TILE = (0, 1), 2, 3
 QUADS = P // SIDE
 LANES = P // SIDE
 BLOCKS = SIDE // LANES
 UNIT = QUADS * LANES
-GROUPS = 2
-GROUP_BLOCKS = BLOCKS // GROUPS
+GROUPS_OF_TILE = 2
+GROUP_BLOCKS = BLOCKS // GROUPS_OF_TILE
 GROUP_COLS = GROUP_BLOCKS * UNIT
-REPEATS = 6
-VECTOR_SUMS = 8
+WIDE, NARROW, WIDE_BLOCKS = 112, 36, 5
 QUARTERS = 4
 QUARTER_SUMS = SIDE // QUARTERS
+VECTOR_SUMS = 16
 TINY = 1e-24
 
 FLOPS = 2 * BATCH * HID * (HID + DOUT)
@@ -277,18 +277,20 @@ def tile_matchingnet_pa_kernel(tc, h3, W4, b4, W5, b5, out):
                     )
                 return bank
 
-            squares = soft.tile([P, DOUT], F32, align_bytes=64, name="squares")
-            by_j = soft.tile([P, DOUT], F32, name="by_j")
-            by_i = soft.tile([P, DOUT], F32, name="by_i")
-            block_banks = [flip_back(BLOCK_TILE, h) for h in range(HALVES)]
-            for h in range(HALVES):
-                nc.vector.transpose(squares[:, BANK * h : BANK * (h + 1)], block_banks[h][:])
-                nc.scalar.copy(
-                    out=by_j[:].rearrange("p (T i x) -> p T i x", T=BLOCKS, x=LANES)[
-                        :, :, HALF_SIDE * h : HALF_SIDE * (h + 1), :
-                    ],
-                    in_=squares[:, BANK * h : BANK * (h + 1)].rearrange("p (i T x) -> p T i x", T=BLOCKS, x=LANES),
-                )
+            by_j = {bt: soft.tile([P, DOUT], F32, name="by_j%d" % bt) for bt in BLOCK_TILES}
+            by_i = {bt: soft.tile([P, DOUT], F32, name="by_i%d" % bt) for bt in BLOCK_TILES}
+            per_bank = BANK // P
+            for bt in BLOCK_TILES:
+                squares = soft.tile([P, DOUT], F32, align_bytes=64, name="squares%d" % bt)
+                for h in range(HALVES):
+                    bank = flip_back(bt, h)
+                    nc.vector.transpose(squares[:, BANK * h : BANK * (h + 1)], bank[:])
+                    nc.scalar.copy(
+                        out=by_j[bt][:].rearrange("p (T i x) -> p T i x", T=BLOCKS, x=LANES)[
+                            :, :, HALF_SIDE * h : HALF_SIDE * (h + 1), :
+                        ],
+                        in_=squares[:, BANK * h : BANK * (h + 1)].rearrange("p (i T x) -> p T i x", T=BLOCKS, x=LANES),
+                    )
             lent_ij = soft.tile([P, DOUT], F32, name="lent_ij")
             lent_ji = soft.tile([P, DOUT], F32, name="lent_ji")
             for h in range(HALVES):
@@ -298,85 +300,86 @@ def tile_matchingnet_pa_kernel(tc, h3, W4, b4, W5, b5, out):
                     in_=bank[:].rearrange("p (i j) -> p j i", j=SIDE),
                 )
                 nc.scalar.copy(out=lent_ij[:, BANK * h : BANK * (h + 1)], in_=bank[:])
-            own_banks = {bt: [flip_back(bt, h) for h in range(HALVES)] for bt in OWN_TILES}
-            per_bank = BANK // P
-            for part in range(BLOCKS // per_bank):
-                bank = banks.tile([P, BANK], F32, tag="bank", name="turned")
-                for q in range(per_bank):
-                    block = per_bank * part + q
-                    nc.tensor.transpose(bank[:, P * q : P * (q + 1)], by_j[:, P * block : P * (block + 1)], ident[:])
-                turned = by_i[:, BANK * part : BANK * (part + 1)]
-                if part == 0:
-                    nc.vector.tensor_copy(out=turned, in_=bank[:])
-                else:
-                    nc.scalar.copy(out=turned, in_=bank[:])
+            own_banks = [flip_back(OWN_TILE, h) for h in range(HALVES)]
+            for bt in BLOCK_TILES:
+                for part in range(BLOCKS // per_bank):
+                    bank = banks.tile([P, BANK], F32, tag="bank", name="turned")
+                    for q in range(per_bank):
+                        block = per_bank * part + q
+                        nc.tensor.transpose(bank[:, P * q : P * (q + 1)], by_j[bt][:, P * block : P * (block + 1)], ident[:])
+                    turned = by_i[bt][:, BANK * part : BANK * (part + 1)]
+                    if part == 0:
+                        nc.vector.tensor_copy(out=turned, in_=bank[:])
+                    else:
+                        nc.scalar.copy(out=turned, in_=bank[:])
             nc.scalar.activation(out=warm[:], in_=tiny[:], func=ACT.Abs_reciprocal_sqrt)
 
             names = ("c", "a")
 
             keep_only = {"c": quad_mask, "a": lane_mask}
-            groups = []
-            for g in range(GROUPS):
+            groups = [(bt, g) for bt in BLOCK_TILES for g in range(GROUPS_OF_TILE)]
+            parts_of = {}
+            for bt, g in groups:
                 parts = {}
                 for name in names:
-                    for kind in ("", "divisor_", "root_"):
-                        parts[kind + name] = soft.tile([P, GROUP_COLS], F32, name="%s%s_g%d" % (kind, name, g))
+                    for kind in ("divisor_", "root_"):
+                        parts[kind + name] = soft.tile([P, GROUP_COLS], F32, name="%s%s_%d%d" % (kind, name, bt, g))
                     nc.gpsimd.memset(parts["divisor_" + name][:], 1.0)
+                    parts[name] = soft.tile([P, GROUP_COLS + WIDE], F32, name="%s_%d%d" % (name, bt, g))
+                    nc.gpsimd.memset(parts[name][:], 0.0)
                 nc.vector.tensor_copy(
-                    out=parts["a"][:].rearrange("p (T x y) -> p T x y", x=LANES, y=QUADS),
+                    out=parts["a"][:, 0:GROUP_COLS].rearrange("p (T x y) -> p T x y", x=LANES, y=QUADS),
                     in_=lane_mask[:].unsqueeze(1).unsqueeze(3).to_broadcast([P, GROUP_BLOCKS, LANES, QUADS]),
                 )
-                parts["sums"] = banks.tile([P, BANK], F32, tag="bank", name="sums_g%d" % g)
-                groups.append(parts)
-            natural = {name: soft.tile([P, P], F32, name="natural_%s" % name) for name in names}
+                parts["sums"] = banks.tile([P, BANK], F32, tag="bank", name="sums_%d%d" % (bt, g))
+                parts_of[bt, g] = parts
+            natural = {
+                (bt, name): soft.tile([P, P], F32, name="natural_%s%d" % (name, bt)) for bt in BLOCK_TILES for name in names
+            }
 
-            def add_up_blocks(g, step):
-                parts = groups[g]
-                blocks, factor = (by_i, parts["a"]) if step % 2 == 0 else (by_j, parts["c"])
+            def add_up_blocks(bt, g, step):
+                parts = parts_of[bt, g]
+                blocks, factor = (by_i[bt], parts["a"]) if step % 2 == 0 else (by_j[bt], parts["c"])
                 for T in range(GROUP_BLOCKS):
                     block = GROUP_BLOCKS * g + T
-                    cols = slice(UNIT * T, UNIT * (T + 1))
-                    columns = factor[:, cols].rearrange("p (u v) -> p v u", u=LANES)
+                    nth = GROUP_BLOCKS * groups.index((bt, g)) + T
+                    cols = slice(UNIT * T, UNIT * T + (WIDE if nth < WIDE_BLOCKS else NARROW))
                     nc.tensor.matmul(
-                        parts["sums"][:, 0 : REPEATS * GROUP_COLS].rearrange("p (r c) -> p r c", r=REPEATS)[:, :, cols],
-                        blocks[:, P * block : P * (block + 1)],
-                        columns.unsqueeze(1).to_broadcast([P, REPEATS, QUADS, LANES]),
-                        start=True,
-                        stop=True,
+                        parts["sums"][:, cols], blocks[:, P * block : P * (block + 1)], factor[:, cols], start=True, stop=True
                     )
 
-            def place(g, name, target):
-                root = groups[g]["root_" + name][:].rearrange("p (T u v) -> p u T v", u=LANES, v=QUADS)
-                for u in range(LANES):
-                    nc.scalar.activation(
-                        out=target[:, u], in_=root[:, u], func=ACT.Square, scale=keep_only[name][:, u : u + 1]
-                    )
-
-            def renew_blocks(g, step):
-                parts = groups[g]
+            def renew_blocks(bt, g, step):
+                parts = parts_of[bt, g]
                 name = names[step % 2]
                 divisor, root = parts["divisor_" + name], parts["root_" + name]
                 nc.vector.scalar_tensor_tensor(
                     out=divisor[:], in0=divisor[:], scalar=EPS, in1=parts["sums"][:, 0:GROUP_COLS], op0=ALU.mult, op1=ALU.max
                 )
                 nc.scalar.activation(out=root[:], in_=divisor[:], func=ACT.Abs_reciprocal_sqrt, bias=tiny[:], scale=1.0)
+                targets = []
                 if step + 1 < STEPS:
-                    place(g, name, parts[name][:].rearrange("p (T u v) -> p u T v", u=LANES, v=QUADS))
+                    targets.append(parts[name][:, 0:GROUP_COLS].rearrange("p (T u v) -> p u T v", u=LANES, v=QUADS))
                 if step + 2 >= STEPS:
                     pattern = "p (u T v) -> p u T v" if name == "c" else "p (v T u) -> p u T v"
-                    columns = natural[name][:].rearrange(pattern, T=BLOCKS, u=LANES)
-                    place(g, name, columns[:, :, GROUP_BLOCKS * g : GROUP_BLOCKS * (g + 1), :])
+                    columns = natural[bt, name][:].rearrange(pattern, T=BLOCKS, u=LANES)
+                    targets.append(columns[:, :, GROUP_BLOCKS * g : GROUP_BLOCKS * (g + 1), :])
+                by_u = root[:].rearrange("p (T v u) -> p u T v", u=LANES, v=QUADS)
+                for target in targets:
+                    for u in range(LANES):
+                        nc.scalar.activation(
+                            out=target[:, u], in_=by_u[:, u], func=ACT.Square, scale=keep_only[name][:, u : u + 1]
+                        )
 
-            def to_rows(name):
-                rows = soft.tile([P, SIDE], F32, name="rows_%s" % name)
-                first = REPEATS * GROUP_COLS + (0 if name == "c" else 2 * SIDE)
-                bank = groups[0]["sums"][:, first : first + SIDE]
-                nc.tensor.matmul(bank, natural[name][:], (pick_j if name == "c" else pick_i)[:], start=True, stop=True)
-                nc.scalar.copy(out=rows[:], in_=bank)
+            def to_rows(bt, name):
+                rows = soft.tile([P, SIDE], F32, name="rows_%s%d" % (name, bt))
+                bank = banks.tile([P, BANK], F32, tag="bank", name="rows_bank")
+                picks = pick_j if name == "c" else pick_i
+                nc.tensor.matmul(bank[:, 0:SIDE], natural[bt, name][:], picks[:], start=True, stop=True)
+                nc.scalar.copy(out=rows[:], in_=bank[:, 0:SIDE])
                 return rows
 
             state = {}
-            for bt in OWN_TILES + (LENT_TILE,):
+            for bt in (OWN_TILE, LENT_TILE):
                 mine = {}
                 for name in names:
                     mine[name] = soft.tile([P, SIDE], F32, name="%s%d" % (name, bt))
@@ -386,13 +389,12 @@ def tile_matchingnet_pa_kernel(tc, h3, W4, b4, W5, b5, out):
                 mine["root"] = soft.tile([P, SIDE], F32, name="root%d" % bt)
                 mine["prod"] = soft.tile([P, DOUT], F32, name="prod%d" % bt)
                 state[bt] = mine
-            for bt in OWN_TILES:
-                nc.vector.memset(state[bt]["a"][:], 1.0)
+            nc.vector.memset(state[OWN_TILE]["a"][:], 1.0)
             unused = soft.tile([P, SIDE, SIDE], F32, name="unused")
 
-            def multiply_own(bt, step):
-                mine = state[bt]
-                for h, bank in enumerate(own_banks[bt]):
+            def multiply_own(step):
+                mine = state[OWN_TILE]
+                for h, bank in enumerate(own_banks):
                     rows = slice(HALF_SIDE * h, HALF_SIDE * (h + 1))
                     if step % 2 == 0:
                         out_view = mine["prod"][:].rearrange("p (j i) -> p j i", i=SIDE)[:, :, rows]
@@ -404,8 +406,8 @@ def tile_matchingnet_pa_kernel(tc, h3, W4, b4, W5, b5, out):
                         factor = mine["c"][:].unsqueeze(1).to_broadcast([P, HALF_SIDE, SIDE])
                     nc.vector.tensor_tensor(out=out_view, in0=in_view, in1=factor, op=ALU.mult)
 
-            def add_up_own(bt, step):
-                mine = state[bt]
+            def add_up_own(step):
+                mine = state[OWN_TILE]
                 nc.vector.tensor_reduce(
                     out=mine["bounds_" + names[step % 2]][:, 0, :],
                     in_=mine["prod"][:].rearrange("p (s t) -> p s t", t=SIDE),
@@ -475,38 +477,38 @@ def tile_matchingnet_pa_kernel(tc, h3, W4, b4, W5, b5, out):
                     )
                 store(LENT_TILE, mine["prod"])
 
-            first_own, second_own = OWN_TILES
-            block_result = soft.tile([P, DOUT], F32, name="block_result")
             with tc.manual_schedule():
                 for step in range(STEPS):
-                    for g in range(GROUPS):
-                        add_up_blocks(g, step)
-                    multiply_own(first_own, step)
+                    for bt, g in groups:
+                        add_up_blocks(bt, g, step)
+                    multiply_own(step)
                     if step > 0:
                         renew(LENT_TILE, step - 1)
                         multiply_lent(step)
-                    renew_blocks(0, step)
-                    add_up_own(first_own, step)
+                    renew_blocks(*groups[0], step)
+                    add_up_own(step)
+                    renew_blocks(*groups[1], step)
                     add_up_lent(step, 0)
-                    add_up_lent(step, 1)
-                    renew(first_own, step)
-                    multiply_own(second_own, step)
+                    renew(OWN_TILE, step)
                     add_up_lent(step, 2)
-                    renew_blocks(1, step)
+                    renew_blocks(*groups[2], step)
                     add_up_lent(step, 3)
-                    add_up_own(second_own, step)
-                    renew(second_own, step)
+                    renew_blocks(*groups[3], step)
                 renew(LENT_TILE, STEPS - 1)
-                rows_c = to_rows("c")
-                rows_a = to_rows("a")
+                rows = {}
+                for name in names:
+                    for bt in BLOCK_TILES:
+                        rows[bt, name] = to_rows(bt, name)
+                finish(OWN_TILE, state[OWN_TILE]["prod"], state[OWN_TILE]["a"])
                 finish_lent()
-                for h in range(HALVES):
-                    nc.vector.tensor_tensor(
-                        out=block_result[:, BANK * h : BANK * (h + 1)].rearrange("p (i j) -> p i j", j=SIDE),
-                        in0=block_banks[h][:].rearrange("p (i j) -> p i j", j=SIDE),
-                        in1=rows_c[:].unsqueeze(1).to_broadcast([P, HALF_SIDE, SIDE]),
-                        op=ALU.mult,
-                    )
-                for bt in OWN_TILES:
-                    finish(bt, state[bt]["prod"], state[bt]["a"])
-                finish(BLOCK_TILE, block_result, rows_a)
+                for bt in BLOCK_TILES:
+                    result = soft.tile([P, DOUT], F32, name="result%d" % bt)
+                    for h in range(HALVES):
+                        bank = flip_back(bt, h)
+                        nc.vector.tensor_tensor(
+                            out=result[:, BANK * h : BANK * (h + 1)].rearrange("p (i j) -> p i j", j=SIDE),
+                            in0=bank[:].rearrange("p (i j) -> p i j", j=SIDE),
+                            in1=rows[bt, "c"][:].unsqueeze(1).to_broadcast([P, HALF_SIDE, SIDE]),
+                            op=ALU.mult,
+                        )
+                    finish(bt, result, rows[bt, "a"])

@@ -46,9 +46,6 @@ GROUPS_OF_TILE = 2
 GROUP_BLOCKS = BLOCKS // GROUPS_OF_TILE
 GROUP_COLS = GROUP_BLOCKS * UNIT
 WIDE, NARROW, WIDE_BLOCKS = 112, 36, 5
-QUARTERS = 4
-QUARTER_SUMS = SIDE // QUARTERS
-VECTOR_SUMS = 16
 TINY = 1e-24
 
 FLOPS = 2 * BATCH * HID * (HID + DOUT)
@@ -390,7 +387,6 @@ def tile_matchingnet_pa_kernel(tc, h3, W4, b4, W5, b5, out):
                 mine["prod"] = soft.tile([P, DOUT], F32, name="prod%d" % bt)
                 state[bt] = mine
             nc.vector.memset(state[OWN_TILE]["a"][:], 1.0)
-            unused = soft.tile([P, SIDE, SIDE], F32, name="unused")
 
             def multiply_own(step):
                 mine = state[OWN_TILE]
@@ -418,32 +414,22 @@ def tile_matchingnet_pa_kernel(tc, h3, W4, b4, W5, b5, out):
             def multiply_lent(step):
                 mine = state[LENT_TILE]
                 matrix, factor = (lent_ji, mine["a"]) if step % 2 == 0 else (lent_ij, mine["c"])
-                for quarter in range(QUARTERS):
-                    rows = slice(QUARTER_SUMS * quarter, QUARTER_SUMS * (quarter + 1))
+                for half in range(2):
+                    rows = slice(HALF_SIDE * half, HALF_SIDE * (half + 1))
                     nc.gpsimd.tensor_tensor(
                         out=mine["prod"][:].rearrange("p (s t) -> p s t", t=SIDE)[:, rows, :],
                         in0=matrix[:].rearrange("p (s t) -> p s t", t=SIDE)[:, rows, :],
-                        in1=factor[:].unsqueeze(1).to_broadcast([P, QUARTER_SUMS, SIDE]),
+                        in1=factor[:].unsqueeze(1).to_broadcast([P, HALF_SIDE, SIDE]),
                         op=ALU.mult,
                     )
 
-            def add_up_lent(step, quarter):
+            def add_up_lent(step, half):
                 mine = state[LENT_TILE]
                 terms = (lent_ji if step == 0 else mine["prod"])[:].rearrange("p (s t) -> p s t", t=SIDE)
-                if quarter == 0:
-                    nc.vector.tensor_reduce(
-                        out=mine["bounds_" + names[step % 2]][:, 0, :VECTOR_SUMS],
-                        in_=terms[:, :VECTOR_SUMS, :],
-                        axis=AXIS.X,
-                        op=ALU.add,
-                    )
-                for s in range(max(VECTOR_SUMS, QUARTER_SUMS * quarter), QUARTER_SUMS * (quarter + 1)):
-                    nc.scalar.activation(
-                        out=unused[:, s, :],
-                        in_=terms[:, s, :],
-                        func=ACT.Copy,
-                        accum_out=mine["bounds_" + names[step % 2]][:, 0, s : s + 1],
-                    )
+                rows = slice(HALF_SIDE * half, HALF_SIDE * (half + 1))
+                nc.vector.tensor_reduce(
+                    out=mine["bounds_" + names[step % 2]][:, 0, rows], in_=terms[:, rows, :], axis=AXIS.X, op=ALU.add
+                )
 
             def renew(bt, step):
                 mine = state[bt]
@@ -479,22 +465,23 @@ def tile_matchingnet_pa_kernel(tc, h3, W4, b4, W5, b5, out):
 
             with tc.manual_schedule():
                 for step in range(STEPS):
-                    for bt, g in groups:
+                    for bt, g in groups[:-1]:
                         add_up_blocks(bt, g, step)
                     multiply_own(step)
                     if step > 0:
-                        renew(LENT_TILE, step - 1)
-                        multiply_lent(step)
-                    renew_blocks(*groups[0], step)
+                        renew_blocks(*groups[-1], step - 1)
+                    add_up_blocks(*groups[-1], step)
                     add_up_own(step)
-                    renew_blocks(*groups[1], step)
-                    add_up_lent(step, 0)
+                    renew_blocks(*groups[0], step)
                     renew(OWN_TILE, step)
-                    add_up_lent(step, 2)
+                    add_up_lent(step, 0)
+                    renew_blocks(*groups[1], step)
+                    add_up_lent(step, 1)
+                    renew(LENT_TILE, step)
+                    if step + 1 < STEPS:
+                        multiply_lent(step + 1)
                     renew_blocks(*groups[2], step)
-                    add_up_lent(step, 3)
-                    renew_blocks(*groups[3], step)
-                renew(LENT_TILE, STEPS - 1)
+                renew_blocks(*groups[-1], STEPS - 1)
                 rows = {}
                 for name in names:
                     for bt in BLOCK_TILES:

@@ -25,12 +25,13 @@ BATCH_TILES = BATCH // P
 BANK = 512
 BANKS = 8
 W_CHUNK = 1024
-CHUNK_TILES = W_CHUNK // P
-AHEAD = 3
-GROUPED_BUFS = 3
+AHEAD = 5
+RAW_BUFS = AHEAD + 3
+UNIT_BUFS = 4
 ACTS_BUFS = 2
+LATE_UNITS = 3
 RUN = 4
-VECTOR_COLS = 448
+B5_ROW = 32
 I_LO = P // SIDE
 D_TILES = DOUT // P
 HALVES = DOUT // BANK
@@ -76,29 +77,38 @@ def tile_matchingnet_pa_kernel(tc, h3, W4, b4, W5, b5, out):
         ):
             nc.vector.tensor_reduce(out=column_sums[:], in_=view, axis=AXIS.X, op=ALU.add)
 
+        expo = consts.tile([P, D_TILES, BATCH], F32, name="expo")
+        r_flipped = consts.tile([P, D_TILES, BATCH], F32, name="r_flipped")
+        bias_rows = consts.tile([P, K_PASS], BF16, name="bias_rows")
+        nc.gpsimd.memset(bias_rows[:], 0.0)
+
         with ExitStack() as front:
             keep = front.enter_context(tc.tile_pool(name="keep", bufs=1))
-            wraw = front.enter_context(tc.tile_pool(name="wraw", bufs=AHEAD + 1))
-            stage = front.enter_context(tc.tile_pool(name="stage", bufs=GROUPED_BUFS))
+            wraw = front.enter_context(tc.tile_pool(name="wraw", bufs=RAW_BUFS))
+            stage = front.enter_context(tc.tile_pool(name="stage", bufs=UNIT_BUFS))
             acts = front.enter_context(tc.tile_pool(name="acts", bufs=ACTS_BUFS))
 
-            chunks = [("w4", block, g) for block in range(HID // W_CHUNK) for g in range(PASSES)]
-            chunks += [("w5", 0, g) for g in range(PASSES)]
+            chunks = [("w4", 0, g) for g in range(PASSES)] + [("w5", 0, g) for g in range(PASSES)]
+            chunks += [("w4", 1, g) for g in range(PASSES)]
             raws = {}
 
-            def load(n):
-                weights, block, g = chunks[n]
+            def load(n, pieces=1):
+                weights, side, g = chunks[n]
                 raw = wraw.tile([P, PACK, W_CHUNK], BF16, name="raw")
-                cols = slice(W_CHUNK * block, W_CHUNK * (block + 1))
-                rows = (W4 if weights == "w4" else W5)[K_PASS * g : K_PASS * (g + 1), cols]
-                nc.sync.dma_start(out=raw[:], in_=rows.rearrange("(p t) w -> p t w", t=PACK))
-                raws[n] = raw
+                rows = (W4 if weights == "w4" else W5)[K_PASS * g : K_PASS * (g + 1), :]
+                rows = rows.rearrange("(p t) w -> p t w", t=PACK)
+                width = W_CHUNK // pieces
+                for piece in range(pieces):
+                    first = W_CHUNK * side + width * piece
+                    nc.sync.dma_start(
+                        out=raw[:, :, width * piece : width * (piece + 1)], in_=rows[:, :, first : first + width]
+                    )
+                raws[chunks[n]] = raw
 
+            load(0, pieces=2)
             h3_rows = [keep.tile([P, HID], BF16, name="h3_rows%d" % bt) for bt in range(BATCH_TILES)]
             for bt in range(BATCH_TILES):
                 nc.sync.dma_start(out=h3_rows[bt][:], in_=h3[bt * P : (bt + 1) * P, :])
-                if bt == BATCH_TILES // 2 - 1:
-                    load(0)
             for n in range(1, AHEAD):
                 load(n)
 
@@ -133,132 +143,152 @@ def tile_matchingnet_pa_kernel(tc, h3, W4, b4, W5, b5, out):
                     out=h3_codes[:, g, :].bitcast(FP8X4), scales=h3_scales[:, g, :], in_=h3_grouped[g][:]
                 )
 
-            b4_rows = HID // P
-            bias_cols = consts.tile([P, b4_rows + D_TILES], F32, name="bias_cols")
-            b4_cols = consts.tile([P, PASSES, PACK], BF16, name="b4_cols")
-            with nc.allow_non_contiguous_dma("runs of four biases"):
-                nc.sync.dma_start(out=b4_cols[:], in_=b4.rearrange("(g p t) -> p g t", p=P, t=PACK))
-            nc.vector.tensor_copy(
-                out=bias_cols[:, 0:b4_rows].rearrange("p (g t) -> p g t", t=PACK), in_=b4_cols[:]
-            )
-            bias_rows = consts.tile([P, P], BF16, name="bias_rows")
-            nc.vector.memset(bias_rows[:], 0.0)
-            nc.sync.dma_start(out=bias_rows[0:D_TILES, :], in_=b5.rearrange("(row col) -> row col", col=P))
-            bias_rows_f32 = consts.tile([P, P], F32, name="bias_rows_f32")
-            nc.vector.tensor_copy(out=bias_rows_f32[:], in_=bias_rows[:])
-            bias_bank = banks.tile([P, P], F32, tag="bank", name="bias_bank")
-            nc.tensor.transpose(bias_bank[:], bias_rows_f32[:], ident[:])
-            nc.vector.tensor_copy(out=bias_cols[:, b4_rows : b4_rows + D_TILES], in_=bias_bank[:, 0:D_TILES])
+            nc.scalar.dma_start(out=bias_rows[0:PASSES, :], in_=b4.rearrange("(g k) -> g k", k=K_PASS))
+            nc.scalar.dma_start(out=bias_rows[B5_ROW : B5_ROW + D_TILES, 0:P], in_=b5.rearrange("(d c) -> d c", c=P))
+            bias_rows_f32 = keep.tile([P, K_PASS], F32, name="bias_rows_f32")
+            nc.gpsimd.tensor_copy(out=bias_rows_f32[:], in_=bias_rows[:])
+            b4_cols = consts.tile([P, PASSES, PACK], F32, name="b4_cols")
+            b5_cols = consts.tile([P, D_TILES], F32, name="b5_cols")
+            b4_bank = banks.tile([P, PACK, P], F32, tag="bank", name="b4_bank")
+            for t in range(PACK):
+                nc.tensor.transpose(b4_bank[:, t, :], bias_rows_f32[:, t::PACK], ident[:])
+            nc.vector.tensor_copy(out=b4_cols[:].rearrange("p g t -> p t g"), in_=b4_bank[:, :, 0:PASSES])
+            b5_bank = banks.tile([P, P], F32, tag="bank", name="b5_bank")
+            nc.tensor.transpose(b5_bank[:], bias_rows_f32[:, 0:P], ident[:])
+            nc.vector.tensor_copy(out=b5_cols[:], in_=b5_bank[:, B5_ROW : B5_ROW + D_TILES])
 
-            w_codes = {
-                "w4": keep.tile([P, PASSES, HID], U32, align_bytes=64, name="w4_codes"),
-                "w5": keep.tile([P, PASSES, DOUT], U32, align_bytes=64, name="w5_codes"),
-            }
-            w_scales = {
-                "w4": keep.tile([P, PASSES, HID], U8, align_bytes=64, name="w4_scales"),
-                "w5": keep.tile([P, PASSES, DOUT], U8, align_bytes=64, name="w5_scales"),
-            }
+            units = [("w4", q, g) for g in range(PASSES) for q in (0, 1)]
+            w5_units = [("w5", h, g) for g in range(PASSES) for h in (0, 1)]
+            units += w5_units[:-LATE_UNITS]
+            units += [("w4", q, g) for q in (2, 3) for g in range(PASSES)]
+            units += w5_units[-LATE_UNITS:]
+            w5_codes = keep.tile([P, PASSES, DOUT], U32, align_bytes=64, name="w5_codes")
+            w5_scales = keep.tile([P, PASSES, DOUT], U8, align_bytes=64, name="w5_scales")
             h4_codes = keep.tile([P, PASSES, BATCH], U32, align_bytes=64, name="h4_codes")
             h4_scales = keep.tile([P, PASSES, BATCH], U8, align_bytes=64, name="h4_scales")
-            moving = {"w4": (h3_codes, h3_scales), "w5": (h4_codes, h4_scales)}
             groupeds = {}
+            sums_of = {}
 
-            def regroup(n):
-                grouped = stage.tile([P, W_CHUNK, PACK], BF16, align_bytes=64, name="grouped")
-                if chunks[n][0] == "w5":
-                    src = raws[n][:].rearrange("p t (w r) -> p w t r", r=RUN)
+            def regroup(unit):
+                weights, part, g = unit
+                side, part = divmod(part, 2)
+                raw = raws[weights, side, g][:, :, K_PASS * part : K_PASS * (part + 1)]
+                grouped = stage.tile([P, K_PASS, PACK], BF16, align_bytes=64, name="grouped")
+                if weights == "w5":
+                    src = raw.rearrange("p t (w r) -> p w t r", r=RUN)
                     dst = grouped[:].rearrange("p (w r) t -> p w t r", r=RUN)
-                    cut = VECTOR_COLS // RUN
-                    nc.vector.tensor_copy(out=dst[:, :cut], in_=src[:, :cut])
-                    nc.scalar.copy(out=dst[:, cut:], in_=src[:, cut:])
                 else:
-                    for half in range(W_CHUNK // K_PASS):
-                        cols = slice(K_PASS * half, K_PASS * (half + 1))
-                        src = raws[n][:, :, cols].rearrange("p t (m s) -> p s m t", s=PACK)
-                        dst = grouped[:, cols, :].rearrange("p (s m) t -> p s m t", s=PACK)
-                        if half == 0:
-                            whole_tiles, rest = divmod(VECTOR_COLS, P)
-                            nc.vector.tensor_copy(out=dst[:, :whole_tiles], in_=src[:, :whole_tiles])
-                            nc.vector.tensor_copy(out=dst[:, whole_tiles, :rest], in_=src[:, whole_tiles, :rest])
-                            nc.scalar.copy(out=dst[:, whole_tiles, rest:], in_=src[:, whole_tiles, rest:])
-                        else:
-                            nc.scalar.copy(out=dst, in_=src)
-                groupeds[n] = grouped
+                    src = raw.rearrange("p t (m s) -> p s m t", s=PACK)
+                    dst = grouped[:].rearrange("p (s m) t -> p s m t", s=PACK)
+                cut = src.shape[1] // 2
+                nc.vector.tensor_copy(out=dst[:, :cut], in_=src[:, :cut])
+                nc.scalar.copy(out=dst[:, cut:], in_=src[:, cut:])
+                groupeds[unit] = grouped
 
-            def quantise_and_multiply(n, sums_banks):
-                weights, block, g = chunks[n]
-                cols = slice(W_CHUNK * block, W_CHUNK * (block + 1))
+            def quantise(unit):
+                weights, part, g = unit
+                if weights == "w5":
+                    cols = slice(K_PASS * part, K_PASS * (part + 1))
+                    codes, scales = w5_codes[:, g, cols], w5_scales[:, g, cols]
+                else:
+                    codes = stage.tile([P, K_PASS], U32, align_bytes=64, name="codes")[:, :]
+                    scales = stage.tile([P, K_PASS], U8, align_bytes=64, name="scales")[:, :]
                 nc.vector.quantize_mx(
-                    out=w_codes[weights][:, g, cols].bitcast(FP8X4),
-                    scales=w_scales[weights][:, g, cols],
-                    in_=groupeds[n][:].rearrange("p w t -> p (w t)"),
+                    out=codes.bitcast(FP8X4), scales=scales, in_=groupeds[unit][:].rearrange("p w t -> p (w t)")
                 )
-                for m in range(CHUNK_TILES):
-                    first = W_CHUNK * block + P * m
+                return codes, scales
+
+            def multiply_w4(q, g, codes, scales):
+                if g == 0 and q % 2 == 0:
+                    for near in (q, q + 1):
+                        sums_of[near] = [banks.tile([P, BANK], F32, tag="bank", name="sums%d" % s) for s in range(PACK)]
+                for s in range(PACK):
                     nc.tensor.matmul_mx(
-                        out=sums_banks[m][:],
-                        lhsT=w_codes[weights][:, g, first : first + P].bitcast(FP8X4),
-                        lhsT_scale=w_scales[weights][:, g, first : first + P],
-                        rhs=moving[weights][0][:, g, :].bitcast(FP8X4),
-                        rhs_scale=moving[weights][1][:, g, :],
+                        out=sums_of[q][s][:],
+                        lhsT=codes[:, P * s : P * (s + 1)].bitcast(FP8X4),
+                        lhsT_scale=scales[:, P * s : P * (s + 1)],
+                        rhs=h3_codes[:, g, :].bitcast(FP8X4),
+                        rhs_scale=h3_scales[:, g, :],
                         start=(g == 0),
                         stop=(g == PASSES - 1),
                     )
 
-            def activate(block, sums_banks):
-                for quad in range(CHUNK_TILES // PACK):
-                    g2 = (CHUNK_TILES // PACK) * block + quad
+            def activate(q, pieces=1):
+                width = BATCH // pieces
+                for piece in range(pieces):
+                    rows = slice(width * piece, width * (piece + 1))
                     biased = acts.tile([P, PACK, BATCH], F32, name="biased")
-                    for t in range(PACK):
-                        m = PACK * g2 + t
+                    for s in range(PACK):
                         nc.scalar.activation(
-                            out=biased[:, t, :],
-                            in_=sums_banks[PACK * quad + t][:],
+                            out=biased[:, s, 0:width],
+                            in_=sums_of[q][s][:, rows],
                             func=ACT.Identity,
-                            bias=bias_cols[:, m : m + 1],
+                            bias=b4_cols[:, q, s : s + 1],
                             scale=1.0,
                         )
                     h4_grouped = acts.tile([P, BATCH, PACK], BF16, align_bytes=64, name="h4_grouped")
-                    by_column = biased[:].rearrange("p t b -> p b t")
+                    by_row = biased[:, :, 0:width].rearrange("p t b -> p b t")
                     nc.vector.scalar_tensor_tensor(
-                        out=h4_grouped[:], in0=by_column, scalar=SLOPE, in1=by_column, op0=ALU.mult, op1=ALU.max
+                        out=h4_grouped[:, 0:width, :], in0=by_row, scalar=SLOPE, in1=by_row, op0=ALU.mult, op1=ALU.max
                     )
                     nc.vector.quantize_mx(
-                        out=h4_codes[:, g2, :].bitcast(FP8X4),
-                        scales=h4_scales[:, g2, :],
-                        in_=h4_grouped[:].rearrange("p b t -> p (b t)"),
+                        out=h4_codes[:, q, rows].bitcast(FP8X4),
+                        scales=h4_scales[:, q, rows],
+                        in_=h4_grouped[:, 0:width, :].rearrange("p b t -> p (b t)"),
                     )
 
-            sums_banks = []
-            for n in range(len(chunks) + 1):
-                if n + AHEAD < len(chunks):
-                    load(n + AHEAD)
-                if n < len(chunks):
-                    regroup(n)
-                if n > 0:
-                    weights, block, g = chunks[n - 1]
-                    if g == 0:
-                        sums_banks = [
-                            banks.tile([P, BANK], F32, tag="bank", name="sums_bank%d" % m) for m in range(CHUNK_TILES)
-                        ]
-                    quantise_and_multiply(n - 1, sums_banks)
-                    if weights == "w4" and g == PASSES - 1:
-                        activate(block, sums_banks)
-            z_banks = sums_banks
+            z_banks = {}
+
+            def multiply_w5(d, q):
+                if q == 0:
+                    z_banks[d] = banks.tile([P, BANK], F32, tag="bank", name="z_bank")
+                nc.tensor.matmul_mx(
+                    out=z_banks[d][:],
+                    lhsT=w5_codes[:, q, P * d : P * (d + 1)].bitcast(FP8X4),
+                    lhsT_scale=w5_scales[:, q, P * d : P * (d + 1)],
+                    rhs=h4_codes[:, q, :].bitcast(FP8X4),
+                    rhs_scale=h4_scales[:, q, :],
+                    start=(q == 0),
+                    stop=(q == PASSES - 1),
+                )
+
+            first_uses = [chunks.index((weights, part // 2, g)) for weights, part, g in units]
+            loaded = AHEAD
+            for n in range(len(units) + 1):
+                if n < len(units):
+                    while loaded < min(first_uses[n] + AHEAD, len(chunks)):
+                        load(loaded)
+                        loaded += 1
+                    regroup(units[n])
+                if n == 0:
+                    continue
+                weights, part, g = units[n - 1]
+                codes, scales = quantise(units[n - 1])
+                if weights == "w4":
+                    multiply_w4(part, g, codes, scales)
+                    if g == PASSES - 1:
+                        activate(part, pieces=1 if part < PASSES - 1 else 2)
+                        if part == 2:
+                            for d in range(D_TILES // 2):
+                                for q in range(PASSES - 1):
+                                    multiply_w5(d, q)
+            for d in range(D_TILES // 2, D_TILES):
+                for q in range(PASSES - 1):
+                    multiply_w5(d, q)
+            for d in range(D_TILES):
+                multiply_w5(d, PASSES - 1)
 
         with ExitStack() as back:
             soft = back.enter_context(tc.tile_pool(name="soft", bufs=1))
 
-            expo = soft.tile([P, D_TILES, BATCH], F32, name="expo")
-            r_flipped = soft.tile([P, D_TILES, BATCH], F32, name="r_flipped")
             for d in range(D_TILES):
-                b5_col = bias_cols[:, b4_rows + d : b4_rows + d + 1]
+                b5_col = b5_cols[:, d : d + 1]
                 nc.vector.tensor_scalar(
                     out=expo[:, d, :], in0=z_banks[d][:], scalar1=b5_col, scalar2=LINEAR_FROM, op0=ALU.add, op1=ALU.min
                 )
                 nc.scalar.activation(out=expo[:, d, :], in_=expo[:, d, :], func=ACT.Exp)
             for d in range(D_TILES):
-                b5_col = bias_cols[:, b4_rows + d : b4_rows + d + 1]
+                b5_col = b5_cols[:, d : d + 1]
                 nc.scalar.activation(out=expo[:, d, :], in_=expo[:, d, :], func=ACT.Ln, bias=1.0, scale=1.0)
                 nc.vector.scalar_tensor_tensor(
                     out=r_flipped[:, d, :], in0=z_banks[d][:], scalar=b5_col, in1=expo[:, d, :], op0=ALU.add, op1=ALU.max
@@ -282,7 +312,7 @@ def tile_matchingnet_pa_kernel(tc, h3, W4, b4, W5, b5, out):
                 for h in range(HALVES):
                     bank = flip_back(bt, h)
                     nc.vector.transpose(squares[:, BANK * h : BANK * (h + 1)], bank[:])
-                    nc.scalar.copy(
+                    nc.gpsimd.tensor_copy(
                         out=by_j[bt][:].rearrange("p (T i x) -> p T i x", T=BLOCKS, x=LANES)[
                             :, :, HALF_SIDE * h : HALF_SIDE * (h + 1), :
                         ],
@@ -292,11 +322,13 @@ def tile_matchingnet_pa_kernel(tc, h3, W4, b4, W5, b5, out):
             lent_ji = soft.tile([P, DOUT], F32, name="lent_ji")
             for h in range(HALVES):
                 bank = flip_back(LENT_TILE, h)
-                nc.vector.tensor_copy(
+                nc.scalar.copy(
                     out=lent_ji[:].rearrange("p (j i) -> p j i", i=SIDE)[:, :, HALF_SIDE * h : HALF_SIDE * (h + 1)],
                     in_=bank[:].rearrange("p (i j) -> p j i", j=SIDE),
                 )
-                nc.scalar.copy(out=lent_ij[:, BANK * h : BANK * (h + 1)], in_=bank[:])
+            nc.gpsimd.tensor_copy(
+                out=lent_ij[:].rearrange("p (i j) -> p i j", j=SIDE), in_=lent_ji[:].rearrange("p (j i) -> p i j", i=SIDE)
+            )
             own_banks = [flip_back(OWN_TILE, h) for h in range(HALVES)]
             for bt in BLOCK_TILES:
                 for part in range(BLOCKS // per_bank):
@@ -369,10 +401,11 @@ def tile_matchingnet_pa_kernel(tc, h3, W4, b4, W5, b5, out):
 
             def to_rows(bt, name):
                 rows = soft.tile([P, SIDE], F32, name="rows_%s%d" % (name, bt))
-                bank = banks.tile([P, BANK], F32, tag="bank", name="rows_bank")
+                first = BANK // 2 if name == "c" else BANK // 2 + P
+                sums = parts_of[bt, GROUPS_OF_TILE - 1]["sums"][:, first : first + SIDE]
                 picks = pick_j if name == "c" else pick_i
-                nc.tensor.matmul(bank[:, 0:SIDE], natural[bt, name][:], picks[:], start=True, stop=True)
-                nc.scalar.copy(out=rows[:], in_=bank[:, 0:SIDE])
+                nc.tensor.matmul(sums, natural[bt, name][:], picks[:], start=True, stop=True)
+                nc.vector.tensor_copy(out=rows[:], in_=sums)
                 return rows
 
             state = {}
@@ -444,24 +477,46 @@ def tile_matchingnet_pa_kernel(tc, h3, W4, b4, W5, b5, out):
                 nc.scalar.activation(out=mine[name][:], in_=mine["root"][:], func=ACT.Square)
                 nc.scalar.mul(out=bounds[:, 1, :], in_=mine["divisor"][:], mul=EPS)
 
-            def store(bt, result):
-                nc.sync.dma_start(out=out[P * bt : P * (bt + 1)].rearrange("b i j -> b (i j)"), in_=result[:])
-
-            def finish(bt, result, a):
-                by_matrix = result[:].rearrange("p (i j) -> p i j", j=SIDE)
-                nc.vector.tensor_tensor(
-                    out=by_matrix, in0=by_matrix, in1=a[:].unsqueeze(2).to_broadcast([P, SIDE, SIDE]), op=ALU.mult
+            def store(bt, result, rows):
+                nc.sync.dma_start(
+                    out=out[P * bt : P * (bt + 1), rows, :].rearrange("b i j -> b (i j)"),
+                    in_=result[:, SIDE * rows.start : SIDE * rows.stop],
                 )
-                store(bt, result)
 
-            def finish_lent():
-                mine = state[LENT_TILE]
+            def finish(bt, result, a, engine):
+                by_matrix = result[:].rearrange("p (i j) -> p i j", j=SIDE)
+                for half in range(2):
+                    rows = slice(HALF_SIDE * half, HALF_SIDE * (half + 1))
+                    engine.tensor_tensor(
+                        out=by_matrix[:, rows, :],
+                        in0=by_matrix[:, rows, :],
+                        in1=a[:, rows].unsqueeze(2).to_broadcast([P, HALF_SIDE, SIDE]),
+                        op=ALU.mult,
+                    )
+                    store(bt, result, rows)
+
+            def finish_on_scalar(bt):
+                mine = state[bt]
                 for i in range(SIDE):
                     row = slice(SIDE * i, SIDE * (i + 1))
                     nc.scalar.activation(
                         out=mine["prod"][:, row], in_=mine["prod"][:, row], func=ACT.Copy, scale=mine["a"][:, i : i + 1]
                     )
-                store(LENT_TILE, mine["prod"])
+                    if (i + 1) % HALF_SIDE == 0:
+                        store(bt, mine["prod"], slice(i + 1 - HALF_SIDE, i + 1))
+
+            results = {bt: soft.tile([P, DOUT], F32, name="result%d" % bt) for bt in BLOCK_TILES}
+
+            def times_c(bt):
+                rows_c = to_rows(bt, "c")
+                for h in range(HALVES):
+                    bank = flip_back(bt, h)
+                    nc.vector.tensor_tensor(
+                        out=results[bt][:, BANK * h : BANK * (h + 1)].rearrange("p (i j) -> p i j", j=SIDE),
+                        in0=bank[:].rearrange("p (i j) -> p i j", j=SIDE),
+                        in1=rows_c[:].unsqueeze(1).to_broadcast([P, HALF_SIDE, SIDE]),
+                        op=ALU.mult,
+                    )
 
             with tc.manual_schedule():
                 for step in range(STEPS):
@@ -482,20 +537,9 @@ def tile_matchingnet_pa_kernel(tc, h3, W4, b4, W5, b5, out):
                         multiply_lent(step + 1)
                     renew_blocks(*groups[2], step)
                 renew_blocks(*groups[-1], STEPS - 1)
-                rows = {}
-                for name in names:
-                    for bt in BLOCK_TILES:
-                        rows[bt, name] = to_rows(bt, name)
-                finish(OWN_TILE, state[OWN_TILE]["prod"], state[OWN_TILE]["a"])
-                finish_lent()
+                finish(LENT_TILE, state[LENT_TILE]["prod"], state[LENT_TILE]["a"], nc.gpsimd)
+                finish_on_scalar(OWN_TILE)
                 for bt in BLOCK_TILES:
-                    result = soft.tile([P, DOUT], F32, name="result%d" % bt)
-                    for h in range(HALVES):
-                        bank = flip_back(bt, h)
-                        nc.vector.tensor_tensor(
-                            out=result[:, BANK * h : BANK * (h + 1)].rearrange("p (i j) -> p i j", j=SIDE),
-                            in0=bank[:].rearrange("p (i j) -> p i j", j=SIDE),
-                            in1=rows[bt, "c"][:].unsqueeze(1).to_broadcast([P, HALF_SIDE, SIDE]),
-                            op=ALU.mult,
-                        )
-                    finish(bt, result, rows[bt, "a"])
+                    times_c(bt)
+                for bt in BLOCK_TILES:
+                    finish(bt, results[bt], to_rows(bt, "a"), nc.vector)

@@ -36,7 +36,7 @@ I_LO = P // SIDE
 D_TILES = DOUT // P
 HALVES = DOUT // BANK
 PER_HALF = BANK // P
-LINEAR_FROM = 30.0
+EXP_MAX = 2.0**43
 HALF_SIDE = SIDE // HALVES
 BLOCK_TILES, OWN_TILE, LENT_TILE = (0, 1), 2, 3
 QUADS = P // SIDE
@@ -47,6 +47,7 @@ GROUPS_OF_TILE = 2
 GROUP_BLOCKS = BLOCKS // GROUPS_OF_TILE
 GROUP_COLS = GROUP_BLOCKS * UNIT
 WIDE, NARROW, WIDE_BLOCKS = 112, 36, 5
+LENT_PIECES = (slice(0, 16), slice(16, 26), slice(26, 32))
 TINY = 1e-24
 
 FLOPS = 2 * BATCH * HID * (HID + DOUT)
@@ -178,11 +179,15 @@ def tile_matchingnet_pa_kernel(tc, h3, W4, b4, W5, b5, out):
                     src = raw.rearrange("p t (w r) -> p w t r", r=RUN)
                     dst = grouped[:].rearrange("p (w r) t -> p w t r", r=RUN)
                 else:
-                    src = raw.rearrange("p t (m s) -> p s m t", s=PACK)
-                    dst = grouped[:].rearrange("p (s m) t -> p s m t", s=PACK)
+                    src = raw.rearrange("p t (m r s) -> p s m t r", s=PACK, r=RUN)
+                    dst = grouped[:].rearrange("p (s m r) t -> p s m t r", s=PACK, r=RUN)
                 cut = src.shape[1] // 2
-                nc.vector.tensor_copy(out=dst[:, :cut], in_=src[:, :cut])
-                nc.scalar.copy(out=dst[:, cut:], in_=src[:, cut:])
+                for engine_copy, share in ((nc.vector.tensor_copy, slice(0, cut)), (nc.scalar.copy, slice(cut, 2 * cut))):
+                    if weights == "w5":
+                        engine_copy(out=dst[:, share], in_=src[:, share])
+                    else:
+                        for s in range(share.start, share.stop):
+                            engine_copy(out=dst[:, s], in_=src[:, s])
                 groupeds[unit] = grouped
 
             def quantise(unit):
@@ -283,10 +288,8 @@ def tile_matchingnet_pa_kernel(tc, h3, W4, b4, W5, b5, out):
 
             for d in range(D_TILES):
                 b5_col = b5_cols[:, d : d + 1]
-                nc.vector.tensor_scalar(
-                    out=expo[:, d, :], in0=z_banks[d][:], scalar1=b5_col, scalar2=LINEAR_FROM, op0=ALU.add, op1=ALU.min
-                )
-                nc.scalar.activation(out=expo[:, d, :], in_=expo[:, d, :], func=ACT.Exp)
+                nc.scalar.activation(out=expo[:, d, :], in_=z_banks[d][:], func=ACT.Exp, bias=b5_col, scale=1.0)
+                nc.vector.tensor_scalar_min(expo[:, d, :], expo[:, d, :], EXP_MAX)
             for d in range(D_TILES):
                 b5_col = b5_cols[:, d : d + 1]
                 nc.scalar.activation(out=expo[:, d, :], in_=expo[:, d, :], func=ACT.Ln, bias=1.0, scale=1.0)
@@ -447,19 +450,17 @@ def tile_matchingnet_pa_kernel(tc, h3, W4, b4, W5, b5, out):
             def multiply_lent(step):
                 mine = state[LENT_TILE]
                 matrix, factor = (lent_ji, mine["a"]) if step % 2 == 0 else (lent_ij, mine["c"])
-                for half in range(2):
-                    rows = slice(HALF_SIDE * half, HALF_SIDE * (half + 1))
+                for rows in LENT_PIECES:
                     nc.gpsimd.tensor_tensor(
                         out=mine["prod"][:].rearrange("p (s t) -> p s t", t=SIDE)[:, rows, :],
                         in0=matrix[:].rearrange("p (s t) -> p s t", t=SIDE)[:, rows, :],
-                        in1=factor[:].unsqueeze(1).to_broadcast([P, HALF_SIDE, SIDE]),
+                        in1=factor[:].unsqueeze(1).to_broadcast([P, rows.stop - rows.start, SIDE]),
                         op=ALU.mult,
                     )
 
-            def add_up_lent(step, half):
+            def add_up_lent(step, rows):
                 mine = state[LENT_TILE]
                 terms = (lent_ji if step == 0 else mine["prod"])[:].rearrange("p (s t) -> p s t", t=SIDE)
-                rows = slice(HALF_SIDE * half, HALF_SIDE * (half + 1))
                 nc.vector.tensor_reduce(
                     out=mine["bounds_" + names[step % 2]][:, 0, rows], in_=terms[:, rows, :], axis=AXIS.X, op=ALU.add
                 )
@@ -529,9 +530,10 @@ def tile_matchingnet_pa_kernel(tc, h3, W4, b4, W5, b5, out):
                     add_up_own(step)
                     renew_blocks(*groups[0], step)
                     renew(OWN_TILE, step)
-                    add_up_lent(step, 0)
+                    add_up_lent(step, LENT_PIECES[0])
                     renew_blocks(*groups[1], step)
-                    add_up_lent(step, 1)
+                    for rows in LENT_PIECES[1:]:
+                        add_up_lent(step, rows)
                     renew(LENT_TILE, step)
                     if step + 1 < STEPS:
                         multiply_lent(step + 1)

@@ -29,6 +29,7 @@ AHEAD = 5
 RAW_BUFS = AHEAD + 3
 UNIT_BUFS = 4
 ACTS_BUFS = 2
+ACTIVATE_BEHIND = 2
 LATE_UNITS = 3
 RUN = 4
 B5_ROW = 32
@@ -43,12 +44,13 @@ QUADS = P // SIDE
 LANES = P // SIDE
 BLOCKS = SIDE // LANES
 UNIT = QUADS * LANES
-GROUPS_OF_TILE = 2
+GROUPS_OF_TILE = 1
 GROUP_BLOCKS = BLOCKS // GROUPS_OF_TILE
 GROUP_COLS = GROUP_BLOCKS * UNIT
-WIDE, NARROW, WIDE_BLOCKS = 112, 36, 5
+WIDE, NARROW, WIDE_BLOCKS = 88, 44, 6
 LENT_PIECES = (slice(0, 16), slice(16, 26), slice(26, 32))
 TINY = 1e-24
+HUGE = 2.0**90
 
 FLOPS = 2 * BATCH * HID * (HID + DOUT)
 
@@ -181,8 +183,9 @@ def tile_matchingnet_pa_kernel(tc, h3, W4, b4, W5, b5, out):
                 else:
                     src = raw.rearrange("p t (m r s) -> p s m t r", s=PACK, r=RUN)
                     dst = grouped[:].rearrange("p (s m r) t -> p s m t r", s=PACK, r=RUN)
-                cut = src.shape[1] // 2
-                for engine_copy, share in ((nc.vector.tensor_copy, slice(0, cut)), (nc.scalar.copy, slice(cut, 2 * cut))):
+                whole_unit = src.shape[1]
+                cut = whole_unit // 2
+                for engine_copy, share in ((nc.vector.tensor_copy, slice(0, cut)), (nc.scalar.copy, slice(cut, whole_unit))):
                     if weights == "w5":
                         engine_copy(out=dst[:, share], in_=src[:, share])
                     else:
@@ -259,6 +262,7 @@ def tile_matchingnet_pa_kernel(tc, h3, W4, b4, W5, b5, out):
 
             first_uses = [chunks.index((weights, part // 2, g)) for weights, part, g in units]
             loaded = AHEAD
+            finished = {}
             for n in range(len(units) + 1):
                 if n < len(units):
                     while loaded < min(first_uses[n] + AHEAD, len(chunks)):
@@ -272,11 +276,13 @@ def tile_matchingnet_pa_kernel(tc, h3, W4, b4, W5, b5, out):
                 if weights == "w4":
                     multiply_w4(part, g, codes, scales)
                     if g == PASSES - 1:
-                        activate(part, pieces=1 if part < PASSES - 1 else 2)
-                        if part == 2:
-                            for d in range(D_TILES // 2):
-                                for q in range(PASSES - 1):
-                                    multiply_w5(d, q)
+                        finished.setdefault(min(n + ACTIVATE_BEHIND, len(units)), []).append(part)
+                for quarter in finished.get(n, []):
+                    activate(quarter, pieces=1 if quarter < PASSES - 1 else 2)
+                    if quarter == 2:
+                        for d in range(D_TILES // 2):
+                            for q in range(PASSES - 1):
+                                multiply_w5(d, q)
             for d in range(D_TILES // 2, D_TILES):
                 for q in range(PASSES - 1):
                     multiply_w5(d, q)
@@ -290,12 +296,19 @@ def tile_matchingnet_pa_kernel(tc, h3, W4, b4, W5, b5, out):
                 b5_col = b5_cols[:, d : d + 1]
                 nc.scalar.activation(out=expo[:, d, :], in_=z_banks[d][:], func=ACT.Exp, bias=b5_col, scale=1.0)
                 nc.vector.tensor_scalar_min(expo[:, d, :], expo[:, d, :], EXP_MAX)
-            for d in range(D_TILES):
+            block_rows, other_rows = slice(0, P * len(BLOCK_TILES)), slice(P * len(BLOCK_TILES), BATCH)
+            pieces = [(d, slice(0, BATCH)) for d in range(PER_HALF)]
+            pieces += [(d, rows) for rows in (block_rows, other_rows) for d in range(PER_HALF, D_TILES)]
+            for d, rows in pieces:
                 b5_col = b5_cols[:, d : d + 1]
-                nc.scalar.activation(out=expo[:, d, :], in_=expo[:, d, :], func=ACT.Ln, bias=1.0, scale=1.0)
+                nc.scalar.activation(out=expo[:, d, rows], in_=expo[:, d, rows], func=ACT.Ln, bias=1.0, scale=1.0)
                 nc.vector.scalar_tensor_tensor(
-                    out=r_flipped[:, d, :], in0=z_banks[d][:], scalar=b5_col, in1=expo[:, d, :], op0=ALU.add, op1=ALU.max
+                    out=r_flipped[:, d, rows], in0=z_banks[d][:, rows], scalar=b5_col, in1=expo[:, d, rows], op0=ALU.add, op1=ALU.max
                 )
+
+            nc.scalar.activation(
+                out=warm[:], in_=expo[:, D_TILES - 1, BATCH - 1 : BATCH], func=ACT.Abs_reciprocal_sqrt, bias=tiny[:], scale=1.0
+            )
 
             def flip_back(bt, h):
                 bank = banks.tile([P, BANK], F32, tag="bank", name="r_bank")
@@ -315,7 +328,7 @@ def tile_matchingnet_pa_kernel(tc, h3, W4, b4, W5, b5, out):
                 for h in range(HALVES):
                     bank = flip_back(bt, h)
                     nc.vector.transpose(squares[:, BANK * h : BANK * (h + 1)], bank[:])
-                    nc.gpsimd.tensor_copy(
+                    (nc.gpsimd if h == 0 else nc.vector).tensor_copy(
                         out=by_j[bt][:].rearrange("p (T i x) -> p T i x", T=BLOCKS, x=LANES)[
                             :, :, HALF_SIDE * h : HALF_SIDE * (h + 1), :
                         ],
@@ -344,19 +357,35 @@ def tile_matchingnet_pa_kernel(tc, h3, W4, b4, W5, b5, out):
                         nc.vector.tensor_copy(out=turned, in_=bank[:])
                     else:
                         nc.scalar.copy(out=turned, in_=bank[:])
-            nc.scalar.activation(out=warm[:], in_=tiny[:], func=ACT.Abs_reciprocal_sqrt)
 
             names = ("c", "a")
 
-            keep_only = {"c": quad_mask, "a": lane_mask}
+            alien = {}
+            for name, mask in (("c", quad_mask), ("a", lane_mask)):
+                alien[name] = soft.tile([P, LANES], F32, name="alien_%s" % name)
+                nc.vector.tensor_scalar(
+                    out=alien[name][:], in0=mask[:], scalar1=-HUGE, scalar2=HUGE, op0=ALU.mult, op1=ALU.add
+                )
             groups = [(bt, g) for bt in BLOCK_TILES for g in range(GROUPS_OF_TILE)]
             parts_of = {}
+
+            def by_factor(columns):
+                return columns.rearrange("p (T u v) -> p u T v", u=LANES, v=QUADS)
+
+            def bound_blocks(parts, name):
+                bounds, divisors = by_factor(parts["bound_" + name][:]), by_factor(parts["divisor_" + name][:])
+                for u in range(LANES):
+                    nc.scalar.activation(
+                        out=bounds[:, u], in_=divisors[:, u], func=ACT.Identity, bias=alien[name][:, u : u + 1], scale=EPS
+                    )
+
             for bt, g in groups:
                 parts = {}
                 for name in names:
-                    for kind in ("divisor_", "root_"):
+                    for kind in ("bound_", "divisor_", "root_"):
                         parts[kind + name] = soft.tile([P, GROUP_COLS], F32, name="%s%s_%d%d" % (kind, name, bt, g))
                     nc.gpsimd.memset(parts["divisor_" + name][:], 1.0)
+                    bound_blocks(parts, name)
                     parts[name] = soft.tile([P, GROUP_COLS + WIDE], F32, name="%s_%d%d" % (name, bt, g))
                     nc.gpsimd.memset(parts[name][:], 0.0)
                 nc.vector.tensor_copy(
@@ -384,23 +413,22 @@ def tile_matchingnet_pa_kernel(tc, h3, W4, b4, W5, b5, out):
                 parts = parts_of[bt, g]
                 name = names[step % 2]
                 divisor, root = parts["divisor_" + name], parts["root_" + name]
-                nc.vector.scalar_tensor_tensor(
-                    out=divisor[:], in0=divisor[:], scalar=EPS, in1=parts["sums"][:, 0:GROUP_COLS], op0=ALU.mult, op1=ALU.max
+                own_order = dict(u=LANES, v=QUADS)
+                nc.vector.tensor_tensor(
+                    out=divisor[:].rearrange("p (T u v) -> p T u v", **own_order),
+                    in0=parts["sums"][:, 0:GROUP_COLS].rearrange("p (T v u) -> p T u v", **own_order),
+                    in1=parts["bound_" + name][:].rearrange("p (T u v) -> p T u v", **own_order),
+                    op=ALU.max,
                 )
                 nc.scalar.activation(out=root[:], in_=divisor[:], func=ACT.Abs_reciprocal_sqrt, bias=tiny[:], scale=1.0)
-                targets = []
                 if step + 1 < STEPS:
-                    targets.append(parts[name][:, 0:GROUP_COLS].rearrange("p (T u v) -> p u T v", u=LANES, v=QUADS))
+                    nc.scalar.activation(out=parts[name][:, 0:GROUP_COLS], in_=root[:], func=ACT.Square)
                 if step + 2 >= STEPS:
                     pattern = "p (u T v) -> p u T v" if name == "c" else "p (v T u) -> p u T v"
                     columns = natural[bt, name][:].rearrange(pattern, T=BLOCKS, u=LANES)
-                    targets.append(columns[:, :, GROUP_BLOCKS * g : GROUP_BLOCKS * (g + 1), :])
-                by_u = root[:].rearrange("p (T v u) -> p u T v", u=LANES, v=QUADS)
-                for target in targets:
-                    for u in range(LANES):
-                        nc.scalar.activation(
-                            out=target[:, u], in_=by_u[:, u], func=ACT.Square, scale=keep_only[name][:, u : u + 1]
-                        )
+                    nc.scalar.activation(
+                        out=columns[:, :, GROUP_BLOCKS * g : GROUP_BLOCKS * (g + 1), :], in_=by_factor(root[:]), func=ACT.Square
+                    )
 
             def to_rows(bt, name):
                 rows = soft.tile([P, SIDE], F32, name="rows_%s%d" % (name, bt))
@@ -484,9 +512,9 @@ def tile_matchingnet_pa_kernel(tc, h3, W4, b4, W5, b5, out):
                     in_=result[:, SIDE * rows.start : SIDE * rows.stop],
                 )
 
-            def finish(bt, result, a, engine):
+            def finish(bt, result, a, engine, halves=(0, 1)):
                 by_matrix = result[:].rearrange("p (i j) -> p i j", j=SIDE)
-                for half in range(2):
+                for half in halves:
                     rows = slice(HALF_SIDE * half, HALF_SIDE * (half + 1))
                     engine.tensor_tensor(
                         out=by_matrix[:, rows, :],
@@ -496,15 +524,12 @@ def tile_matchingnet_pa_kernel(tc, h3, W4, b4, W5, b5, out):
                     )
                     store(bt, result, rows)
 
-            def finish_on_scalar(bt):
-                mine = state[bt]
-                for i in range(SIDE):
-                    row = slice(SIDE * i, SIDE * (i + 1))
-                    nc.scalar.activation(
-                        out=mine["prod"][:, row], in_=mine["prod"][:, row], func=ACT.Copy, scale=mine["a"][:, i : i + 1]
-                    )
-                    if (i + 1) % HALF_SIDE == 0:
-                        store(bt, mine["prod"], slice(i + 1 - HALF_SIDE, i + 1))
+            def finish_on_scalar(bt, result, a, half):
+                rows = slice(HALF_SIDE * half, HALF_SIDE * (half + 1))
+                for i in range(rows.start, rows.stop):
+                    row = result[:, SIDE * i : SIDE * (i + 1)]
+                    nc.scalar.activation(out=row, in_=row, func=ACT.Copy, scale=a[:, i : i + 1])
+                store(bt, result, rows)
 
             results = {bt: soft.tile([P, DOUT], F32, name="result%d" % bt) for bt in BLOCK_TILES}
 
@@ -521,15 +546,13 @@ def tile_matchingnet_pa_kernel(tc, h3, W4, b4, W5, b5, out):
 
             with tc.manual_schedule():
                 for step in range(STEPS):
-                    for bt, g in groups[:-1]:
+                    for bt, g in groups:
                         add_up_blocks(bt, g, step)
                     multiply_own(step)
-                    if step > 0:
-                        renew_blocks(*groups[-1], step - 1)
-                    add_up_blocks(*groups[-1], step)
-                    add_up_own(step)
                     renew_blocks(*groups[0], step)
+                    add_up_own(step)
                     renew(OWN_TILE, step)
+                    bound_blocks(parts_of[groups[0]], names[step % 2])
                     add_up_lent(step, LENT_PIECES[0])
                     renew_blocks(*groups[1], step)
                     for rows in LENT_PIECES[1:]:
@@ -537,11 +560,14 @@ def tile_matchingnet_pa_kernel(tc, h3, W4, b4, W5, b5, out):
                     renew(LENT_TILE, step)
                     if step + 1 < STEPS:
                         multiply_lent(step + 1)
-                    renew_blocks(*groups[2], step)
-                renew_blocks(*groups[-1], STEPS - 1)
+                    bound_blocks(parts_of[groups[1]], names[step % 2])
+                for half in range(2):
+                    finish_on_scalar(OWN_TILE, state[OWN_TILE]["prod"], state[OWN_TILE]["a"], half)
                 finish(LENT_TILE, state[LENT_TILE]["prod"], state[LENT_TILE]["a"], nc.gpsimd)
-                finish_on_scalar(OWN_TILE)
                 for bt in BLOCK_TILES:
                     times_c(bt)
-                for bt in BLOCK_TILES:
-                    finish(bt, results[bt], to_rows(bt, "a"), nc.vector)
+                rows_a = {bt: to_rows(bt, "a") for bt in BLOCK_TILES}
+                first, last = BLOCK_TILES
+                finish(first, results[first], rows_a[first], nc.vector)
+                finish(last, results[last], rows_a[last], nc.vector, halves=(0,))
+                finish_on_scalar(last, results[last], rows_a[last], 1)

@@ -48,7 +48,7 @@ GROUPS_OF_TILE = 1
 GROUP_BLOCKS = BLOCKS // GROUPS_OF_TILE
 GROUP_COLS = GROUP_BLOCKS * UNIT
 WIDE, NARROW, WIDE_BLOCKS = 88, 44, 6
-LENT_PIECES = (slice(0, 16), slice(16, 26), slice(26, 32))
+LENT_PIECES = (slice(0, 22), slice(22, 32))
 TINY = 1e-24
 HUGE = 2.0**90
 
@@ -409,10 +409,10 @@ def tile_matchingnet_pa_kernel(tc, h3, W4, b4, W5, b5, out):
                         parts["sums"][:, cols], blocks[:, P * block : P * (block + 1)], factor[:, cols], start=True, stop=True
                     )
 
-            def renew_blocks(bt, g, step):
+            def divide_blocks(bt, g, step):
                 parts = parts_of[bt, g]
                 name = names[step % 2]
-                divisor, root = parts["divisor_" + name], parts["root_" + name]
+                divisor = parts["divisor_" + name]
                 own_order = dict(u=LANES, v=QUADS)
                 nc.vector.tensor_tensor(
                     out=divisor[:].rearrange("p (T u v) -> p T u v", **own_order),
@@ -420,6 +420,11 @@ def tile_matchingnet_pa_kernel(tc, h3, W4, b4, W5, b5, out):
                     in1=parts["bound_" + name][:].rearrange("p (T u v) -> p T u v", **own_order),
                     op=ALU.max,
                 )
+
+            def renew_blocks(bt, g, step):
+                parts = parts_of[bt, g]
+                name = names[step % 2]
+                divisor, root = parts["divisor_" + name], parts["root_" + name]
                 nc.scalar.activation(out=root[:], in_=divisor[:], func=ACT.Abs_reciprocal_sqrt, bias=tiny[:], scale=1.0)
                 if step + 1 < STEPS:
                     nc.scalar.activation(out=parts[name][:, 0:GROUP_COLS], in_=root[:], func=ACT.Square)
@@ -429,6 +434,8 @@ def tile_matchingnet_pa_kernel(tc, h3, W4, b4, W5, b5, out):
                     nc.scalar.activation(
                         out=columns[:, :, GROUP_BLOCKS * g : GROUP_BLOCKS * (g + 1), :], in_=by_factor(root[:]), func=ACT.Square
                     )
+                if step + 2 < STEPS:
+                    bound_blocks(parts, name)
 
             def to_rows(bt, name):
                 rows = soft.tile([P, SIDE], F32, name="rows_%s%d" % (name, bt))
@@ -549,18 +556,18 @@ def tile_matchingnet_pa_kernel(tc, h3, W4, b4, W5, b5, out):
                     for bt, g in groups:
                         add_up_blocks(bt, g, step)
                     multiply_own(step)
+                    divide_blocks(*groups[0], step)
                     renew_blocks(*groups[0], step)
                     add_up_own(step)
-                    renew(OWN_TILE, step)
-                    bound_blocks(parts_of[groups[0]], names[step % 2])
                     add_up_lent(step, LENT_PIECES[0])
-                    renew_blocks(*groups[1], step)
+                    renew(OWN_TILE, step)
                     for rows in LENT_PIECES[1:]:
                         add_up_lent(step, rows)
+                    divide_blocks(*groups[1], step)
                     renew(LENT_TILE, step)
                     if step + 1 < STEPS:
                         multiply_lent(step + 1)
-                    bound_blocks(parts_of[groups[1]], names[step % 2])
+                    renew_blocks(*groups[1], step)
                 for half in range(2):
                     finish_on_scalar(OWN_TILE, state[OWN_TILE]["prod"], state[OWN_TILE]["a"], half)
                 finish(LENT_TILE, state[LENT_TILE]["prod"], state[LENT_TILE]["a"], nc.gpsimd)

@@ -44,7 +44,7 @@ QUADS = P // SIDE
 LANES = P // SIDE
 BLOCKS = SIDE // LANES
 UNIT = QUADS * LANES
-GROUPS_OF_TILE = 1
+GROUPS_OF_TILE = 2
 GROUP_BLOCKS = BLOCKS // GROUPS_OF_TILE
 GROUP_COLS = GROUP_BLOCKS * UNIT
 WIDE, NARROW, WIDE_BLOCKS = 88, 44, 6
@@ -434,8 +434,6 @@ def tile_matchingnet_pa_kernel(tc, h3, W4, b4, W5, b5, out):
                     nc.scalar.activation(
                         out=columns[:, :, GROUP_BLOCKS * g : GROUP_BLOCKS * (g + 1), :], in_=by_factor(root[:]), func=ACT.Square
                     )
-                if step + 2 < STEPS:
-                    bound_blocks(parts, name)
 
             def to_rows(bt, name):
                 rows = soft.tile([P, SIDE], F32, name="rows_%s%d" % (name, bt))
@@ -553,21 +551,33 @@ def tile_matchingnet_pa_kernel(tc, h3, W4, b4, W5, b5, out):
 
             with tc.manual_schedule():
                 for step in range(STEPS):
-                    for bt, g in groups:
+                    for bt, g in groups[:-1]:
                         add_up_blocks(bt, g, step)
                     multiply_own(step)
+                    if step > 0:
+                        divide_blocks(*groups[-1], step - 1)
+                        renew_blocks(*groups[-1], step - 1)
+                    add_up_blocks(*groups[-1], step)
+                    add_up_own(step)
                     divide_blocks(*groups[0], step)
                     renew_blocks(*groups[0], step)
-                    add_up_own(step)
-                    add_up_lent(step, LENT_PIECES[0])
                     renew(OWN_TILE, step)
-                    for rows in LENT_PIECES[1:]:
-                        add_up_lent(step, rows)
+                    if 0 < step < STEPS - 1:
+                        bound_blocks(parts_of[groups[-1]], names[(step - 1) % 2])
+                    add_up_lent(step, LENT_PIECES[0])
                     divide_blocks(*groups[1], step)
+                    renew_blocks(*groups[1], step)
+                    add_up_lent(step, LENT_PIECES[1])
+                    divide_blocks(*groups[2], step)
                     renew(LENT_TILE, step)
                     if step + 1 < STEPS:
                         multiply_lent(step + 1)
-                    renew_blocks(*groups[1], step)
+                    renew_blocks(*groups[2], step)
+                    if step + 2 < STEPS:
+                        for group in groups[:-1]:
+                            bound_blocks(parts_of[group], names[step % 2])
+                divide_blocks(*groups[-1], STEPS - 1)
+                renew_blocks(*groups[-1], STEPS - 1)
                 for half in range(2):
                     finish_on_scalar(OWN_TILE, state[OWN_TILE]["prod"], state[OWN_TILE]["a"], half)
                 finish(LENT_TILE, state[LENT_TILE]["prod"], state[LENT_TILE]["a"], nc.gpsimd)

from contextlib import ExitStack

import concourse.mybir as mybir
from concourse.masks import make_identity

F32 = mybir.dt.float32
BF16 = mybir.dt.bfloat16
U32 = mybir.dt.uint32
U8 = mybir.dt.uint8
FP8X4 = mybir.dt.float8_e4m3fn_x4
ALU = mybir.AluOpType
ACT = mybir.ActivationFunctionType
AXIS = mybir.AxisListType

P = 128
PACK = 4
K_PASS = P * PACK
BATCH, SIDE, HID, ROUNDS = 512, 32, 2048, 10
STEPS = 2 * ROUNDS
DOUT = SIDE * SIDE
SLOPE = 0.01
EPS = 1e-8
PASSES = HID // K_PASS
BATCH_TILES = BATCH // P
BANK = 512
BANKS = 8
W_CHUNK = 1024
AHEAD = 5
RAW_BUFS = AHEAD + 3
UNIT_BUFS = 4
ACTS_BUFS = 2
ACTIVATE_BEHIND = 2
LATE_UNITS = 3
RUN = 4
B5_ROW = 32
I_LO = P // SIDE
D_TILES = DOUT // P
HALVES = DOUT // BANK
PER_HALF = BANK // P
EXP_MAX = 2.0**43
HALF_SIDE = SIDE // HALVES
BLOCK_TILES, OWN_TILE, LENT_TILE = (0, 1), 2, 3
QUADS = P // SIDE
LANES = P // SIDE
BLOCKS = SIDE // LANES
UNIT = QUADS * LANES
GROUPS_OF_TILE = 2
GROUP_BLOCKS = BLOCKS // GROUPS_OF_TILE
GROUP_COLS = GROUP_BLOCKS * UNIT
WIDE, NARROW, WIDE_BLOCKS = 88, 44, 6
LENT_PIECES = (slice(0, 22), slice(22, 32))
TINY = 1e-24
HUGE = 2.0**90

FLOPS = 2 * BATCH * HID * (HID + DOUT)


def tile_matchingnet_pa_kernel(tc, h3, W4, b4, W5, b5, out):
    nc = tc.nc
    with ExitStack() as whole:
        consts = whole.enter_context(tc.tile_pool(name="consts", bufs=1))
        banks = whole.enter_context(tc.psum_pool(name="banks", bufs=BANKS))

        tiny = consts.tile([P, 1], F32, name="tiny")
        nc.vector.memset(tiny[:], TINY)
        warm = consts.tile([P, 1], F32, name="warm")
        nc.scalar.activation(out=warm[:], in_=tiny[:], func=ACT.Exp)

        ident = consts.tile([P, P], F32, name="ident")
        make_identity(nc, ident[:])
        lane_mask = consts.tile([P, LANES], F32, name="lane_mask")
        quad_mask = consts.tile([P, QUADS], F32, name="quad_mask")
        pick_i = consts.tile([P, SIDE], F32, name="pick_i")
        pick_j = consts.tile([P, SIDE], F32, name="pick_j")
        for column_sums, view in (
            (lane_mask, ident[:].rearrange("p (i x) -> p x i", x=LANES)),
            (quad_mask, ident[:].rearrange("p (y j) -> p y j", y=QUADS)),
            (pick_i, ident[:].rearrange("p (i x) -> p i x", x=LANES)),
            (pick_j, ident[:].rearrange("p (y j) -> p j y", y=QUADS)),
        ):
            nc.vector.tensor_reduce(out=column_sums[:], in_=view, axis=AXIS.X, op=ALU.add)

        expo = consts.tile([P, D_TILES, BATCH], F32, name="expo")
        r_flipped = consts.tile([P, D_TILES, BATCH], F32, name="r_flipped")
        bias_rows = consts.tile([P, K_PASS], BF16, name="bias_rows")
        nc.gpsimd.memset(bias_rows[:], 0.0)

        with ExitStack() as front:
            keep = front.enter_context(tc.tile_pool(name="keep", bufs=1))
            wraw = front.enter_context(tc.tile_pool(name="wraw", bufs=RAW_BUFS))
            stage = front.enter_context(tc.tile_pool(name="stage", bufs=UNIT_BUFS))
            acts = front.enter_context(tc.tile_pool(name="acts", bufs=ACTS_BUFS))

            chunks = [("w4", 0, g) for g in range(PASSES)] + [("w5", 0, g) for g in range(PASSES)]
            chunks += [("w4", 1, g) for g in range(PASSES)]
            raws = {}

            def load(n, pieces=1):
                weights, side, g = chunks[n]
                raw = wraw.tile([P, PACK, W_CHUNK], BF16, name="raw")
                rows = (W4 if weights == "w4" else W5)[K_PASS * g : K_PASS * (g + 1), :]
                rows = rows.rearrange("(p t) w -> p t w", t=PACK)
                width = W_CHUNK // pieces
                for piece in range(pieces):
                    first = W_CHUNK * side + width * piece
                    nc.sync.dma_start(
                        out=raw[:, :, width * piece : width * (piece + 1)], in_=rows[:, :, first : first + width]
                    )
                raws[chunks[n]] = raw

            load(0, pieces=2)
            h3_rows = [keep.tile([P, HID], BF16, name="h3_rows%d" % bt) for bt in range(BATCH_TILES)]
            for bt in range(BATCH_TILES):
                nc.sync.dma_start(out=h3_rows[bt][:], in_=h3[bt * P : (bt + 1) * P, :])
            for n in range(1, AHEAD):
                load(n)

            h3_grouped = [
                keep.tile([P, BATCH * PACK], BF16, align_bytes=64, name="h3_grouped%d" % g) for g in range(PASSES)
            ]
            h3_codes = keep.tile([P, PASSES, BATCH], U32, align_bytes=64, name="h3_codes")
            h3_scales = keep.tile([P, PASSES, BATCH], U8, align_bytes=64, name="h3_scales")
            for pair in range(BATCH_TILES // 2):
                for g in range(PASSES):
                    flipped = banks.tile([P, 2, 2, P], F32, tag="bank", name="flipped")
                    for member in range(2):
                        words = h3_rows[2 * pair + member][:].bitcast(F32)
                        for u in range(2):
                            first = (K_PASS // 2) * g
                            nc.tensor.transpose(
                                flipped[:, member, u, :], words[:, first + u : first + K_PASS // 2 : 2], ident[:]
                            )
                    dst = (
                        h3_grouped[g][:]
                        .bitcast(F32)
                        .rearrange("p (b u) -> p b u", u=2)[:, 2 * P * pair : 2 * P * (pair + 1), :]
                        .rearrange("p (y b) u -> p y b u", y=2)
                    )
                    src = flipped[:].rearrange("p y u b -> p y b u")
                    if g % 2 == 0:
                        nc.vector.tensor_copy(out=dst, in_=src)
                    else:
                        nc.scalar.copy(out=dst, in_=src)
            for g in range(PASSES):
                nc.vector.quantize_mx(
                    out=h3_codes[:, g, :].bitcast(FP8X4), scales=h3_scales[:, g, :], in_=h3_grouped[g][:]
                )

            nc.scalar.dma_start(out=bias_rows[0:PASSES, :], in_=b4.rearrange("(g k) -> g k", k=K_PASS))
            nc.scalar.dma_start(out=bias_rows[B5_ROW : B5_ROW + D_TILES, 0:P], in_=b5.rearrange("(d c) -> d c", c=P))
            bias_rows_f32 = keep.tile([P, K_PASS], F32, name="bias_rows_f32")
            nc.gpsimd.tensor_copy(out=bias_rows_f32[:], in_=bias_rows[:])
            b4_cols = consts.tile([P, PASSES, PACK], F32, name="b4_cols")
            b5_cols = consts.tile([P, D_TILES], F32, name="b5_cols")
            b4_bank = banks.tile([P, PACK, P], F32, tag="bank", name="b4_bank")
            for t in range(PACK):
                nc.tensor.transpose(b4_bank[:, t, :], bias_rows_f32[:, t::PACK], ident[:])
            nc.vector.tensor_copy(out=b4_cols[:].rearrange("p g t -> p t g"), in_=b4_bank[:, :, 0:PASSES])
            b5_bank = banks.tile([P, P], F32, tag="bank", name="b5_bank")
            nc.tensor.transpose(b5_bank[:], bias_rows_f32[:, 0:P], ident[:])
            nc.vector.tensor_copy(out=b5_cols[:], in_=b5_bank[:, B5_ROW : B5_ROW + D_TILES])

            units = [("w4", q, g) for g in range(PASSES) for q in (0, 1)]
            w5_units = [("w5", h, g) for g in range(PASSES) for h in (0, 1)]
            units += w5_units[:-LATE_UNITS]
            units += [("w4", q, g) for q in (2, 3) for g in range(PASSES)]
            units += w5_units[-LATE_UNITS:]
            w5_codes = keep.tile([P, PASSES, DOUT], U32, align_bytes=64, name="w5_codes")
            w5_scales = keep.tile([P, PASSES, DOUT], U8, align_bytes=64, name="w5_scales")
            h4_codes = keep.tile([P, PASSES, BATCH], U32, align_bytes=64, name="h4_codes")
            h4_scales = keep.tile([P, PASSES, BATCH], U8, align_bytes=64, name="h4_scales")
            groupeds = {}
            sums_of = {}

            def regroup(unit):
                weights, part, g = unit
                side, part = divmod(part, 2)
                raw = raws[weights, side, g][:, :, K_PASS * part : K_PASS * (part + 1)]
                grouped = stage.tile([P, K_PASS, PACK], BF16, align_bytes=64, name="grouped")
                if weights == "w5":
                    src = raw.rearrange("p t (w r) -> p w t r", r=RUN)
                    dst = grouped[:].rearrange("p (w r) t -> p w t r", r=RUN)
                else:
                    src = raw.rearrange("p t (m r s) -> p s m t r", s=PACK, r=RUN)
                    dst = grouped[:].rearrange("p (s m r) t -> p s m t r", s=PACK, r=RUN)
                whole_unit = src.shape[1]
                cut = whole_unit // 2
                for engine_copy, share in ((nc.vector.tensor_copy, slice(0, cut)), (nc.scalar.copy, slice(cut, whole_unit))):
                    if weights == "w5":
                        engine_copy(out=dst[:, share], in_=src[:, share])
                    else:
                        for s in range(share.start, share.stop):
                            engine_copy(out=dst[:, s], in_=src[:, s])
                groupeds[unit] = grouped

            def quantise(unit):
                weights, part, g = unit
                if weights == "w5":
                    cols = slice(K_PASS * part, K_PASS * (part + 1))
                    codes, scales = w5_codes[:, g, cols], w5_scales[:, g, cols]
                else:
                    codes = stage.tile([P, K_PASS], U32, align_bytes=64, name="codes")[:, :]
                    scales = stage.tile([P, K_PASS], U8, align_bytes=64, name="scales")[:, :]
                nc.vector.quantize_mx(
                    out=codes.bitcast(FP8X4), scales=scales, in_=groupeds[unit][:].rearrange("p w t -> p (w t)")
                )
                return codes, scales

            def multiply_w4(q, g, codes, scales):
                if g == 0 and q % 2 == 0:
                    for near in (q, q + 1):
                        sums_of[near] = [banks.tile([P, BANK], F32, tag="bank", name="sums%d" % s) for s in range(PACK)]
                for s in range(PACK):
                    nc.tensor.matmul_mx(
                        out=sums_of[q][s][:],
                        lhsT=codes[:, P * s : P * (s + 1)].bitcast(FP8X4),
                        lhsT_scale=scales[:, P * s : P * (s + 1)],
                        rhs=h3_codes[:, g, :].bitcast(FP8X4),
                        rhs_scale=h3_scales[:, g, :],
                        start=(g == 0),
                        stop=(g == PASSES - 1),
                    )

            def activate(q, pieces=1):
                width = BATCH // pieces
                for piece in range(pieces):
                    rows = slice(width * piece, width * (piece + 1))
                    biased = acts.tile([P, PACK, BATCH], F32, name="biased")
                    for s in range(PACK):
                        nc.scalar.activation(
                            out=biased[:, s, 0:width],
                            in_=sums_of[q][s][:, rows],
                            func=ACT.Identity,
                            bias=b4_cols[:, q, s : s + 1],
                            scale=1.0,
                        )
                    h4_grouped = acts.tile([P, BATCH, PACK], BF16, align_bytes=64, name="h4_grouped")
                    by_row = biased[:, :, 0:width].rearrange("p t b -> p b t")
                    nc.vector.scalar_tensor_tensor(
                        out=h4_grouped[:, 0:width, :], in0=by_row, scalar=SLOPE, in1=by_row, op0=ALU.mult, op1=ALU.max
                    )
                    nc.vector.quantize_mx(
                        out=h4_codes[:, q, rows].bitcast(FP8X4),
                        scales=h4_scales[:, q, rows],
                        in_=h4_grouped[:, 0:width, :].rearrange("p b t -> p (b t)"),
                    )

            z_banks = {}

            def multiply_w5(d, q):
                if q == 0:
                    z_banks[d] = banks.tile([P, BANK], F32, tag="bank", name="z_bank")
                nc.tensor.matmul_mx(
                    out=z_banks[d][:],
                    lhsT=w5_codes[:, q, P * d : P * (d + 1)].bitcast(FP8X4),
                    lhsT_scale=w5_scales[:, q, P * d : P * (d + 1)],
                    rhs=h4_codes[:, q, :].bitcast(FP8X4),
                    rhs_scale=h4_scales[:, q, :],
                    start=(q == 0),
                    stop=(q == PASSES - 1),
                )

            first_uses = [chunks.index((weights, part // 2, g)) for weights, part, g in units]
            loaded = AHEAD
            finished = {}
            for n in range(len(units) + 1):
                if n < len(units):
                    while loaded < min(first_uses[n] + AHEAD, len(chunks)):
                        load(loaded)
                        loaded += 1
                    regroup(units[n])
                if n == 0:
                    continue
                weights, part, g = units[n - 1]
                codes, scales = quantise(units[n - 1])
                if weights == "w4":
                    multiply_w4(part, g, codes, scales)
                    if g == PASSES - 1:
                        finished.setdefault(min(n + ACTIVATE_BEHIND, len(units)), []).append(part)
                for quarter in finished.get(n, []):
                    activate(quarter, pieces=1 if quarter < PASSES - 1 else 2)
                    if quarter == 2:
                        for d in range(D_TILES // 2):
                            for q in range(PASSES - 1):
                                multiply_w5(d, q)
            for d in range(D_TILES // 2, D_TILES):
                for q in range(PASSES - 1):
                    multiply_w5(d, q)
            for d in range(D_TILES):
                multiply_w5(d, PASSES - 1)

        with ExitStack() as back:
            soft = back.enter_context(tc.tile_pool(name="soft", bufs=1))

            for d in range(D_TILES):
                b5_col = b5_cols[:, d : d + 1]
                nc.scalar.activation(out=expo[:, d, :], in_=z_banks[d][:], func=ACT.Exp, bias=b5_col, scale=1.0)
                nc.vector.tensor_scalar_min(expo[:, d, :], expo[:, d, :], EXP_MAX)
            block_rows, other_rows = slice(0, P * len(BLOCK_TILES)), slice(P * len(BLOCK_TILES), BATCH)
            pieces = [(d, slice(0, BATCH)) for d in range(PER_HALF)]
            pieces += [(d, rows) for rows in (block_rows, other_rows) for d in range(PER_HALF, D_TILES)]
            for d, rows in pieces:
                b5_col = b5_cols[:, d : d + 1]
                nc.scalar.activation(out=expo[:, d, rows], in_=expo[:, d, rows], func=ACT.Ln, bias=1.0, scale=1.0)
                nc.vector.scalar_tensor_tensor(
                    out=r_flipped[:, d, rows], in0=z_banks[d][:, rows], scalar=b5_col, in1=expo[:, d, rows], op0=ALU.add, op1=ALU.max
                )

            nc.scalar.activation(
                out=warm[:], in_=expo[:, D_TILES - 1, BATCH - 1 : BATCH], func=ACT.Abs_reciprocal_sqrt, bias=tiny[:], scale=1.0
            )

            def flip_back(bt, h):
                bank = banks.tile([P, BANK], F32, tag="bank", name="r_bank")
                for part in range(PER_HALF):
                    nc.tensor.transpose(
                        bank[:, P * part : P * (part + 1)],
                        r_flipped[:, PER_HALF * h + part, P * bt : P * (bt + 1)],
                        ident[:],
                    )
                return bank

            by_j = {bt: soft.tile([P, DOUT], F32, name="by_j%d" % bt) for bt in BLOCK_TILES}
            by_i = {bt: soft.tile([P, DOUT], F32, name="by_i%d" % bt) for bt in BLOCK_TILES}
            per_bank = BANK // P
            for bt in BLOCK_TILES:
                squares = soft.tile([P, DOUT], F32, align_bytes=64, name="squares%d" % bt)
                for h in range(HALVES):
                    bank = flip_back(bt, h)
                    nc.vector.transpose(squares[:, BANK * h : BANK * (h + 1)], bank[:])
                    (nc.gpsimd if h == 0 else nc.vector).tensor_copy(
                        out=by_j[bt][:].rearrange("p (T i x) -> p T i x", T=BLOCKS, x=LANES)[
                            :, :, HALF_SIDE * h : HALF_SIDE * (h + 1), :
                        ],
                        in_=squares[:, BANK * h : BANK * (h + 1)].rearrange("p (i T x) -> p T i x", T=BLOCKS, x=LANES),
                    )
            lent_ij = soft.tile([P, DOUT], F32, name="lent_ij")
            lent_ji = soft.tile([P, DOUT], F32, name="lent_ji")
            for h in range(HALVES):
                bank = flip_back(LENT_TILE, h)
                nc.scalar.copy(
                    out=lent_ji[:].rearrange("p (j i) -> p j i", i=SIDE)[:, :, HALF_SIDE * h : HALF_SIDE * (h + 1)],
                    in_=bank[:].rearrange("p (i j) -> p j i", j=SIDE),
                )
            nc.gpsimd.tensor_copy(
                out=lent_ij[:].rearrange("p (i j) -> p i j", j=SIDE), in_=lent_ji[:].rearrange("p (j i) -> p i j", i=SIDE)
            )
            own_banks = [flip_back(OWN_TILE, h) for h in range(HALVES)]
            for bt in BLOCK_TILES:
                for part in range(BLOCKS // per_bank):
                    bank = banks.tile([P, BANK], F32, tag="bank", name="turned")
                    for q in range(per_bank):
                        block = per_bank * part + q
                        nc.tensor.transpose(bank[:, P * q : P * (q + 1)], by_j[bt][:, P * block : P * (block + 1)], ident[:])
                    turned = by_i[bt][:, BANK * part : BANK * (part + 1)]
                    if part == 0:
                        nc.vector.tensor_copy(out=turned, in_=bank[:])
                    else:
                        nc.scalar.copy(out=turned, in_=bank[:])

            names = ("c", "a")

            alien = {}
            for name, mask in (("c", quad_mask), ("a", lane_mask)):
                alien[name] = soft.tile([P, LANES], F32, name="alien_%s" % name)
                nc.vector.tensor_scalar(
                    out=alien[name][:], in0=mask[:], scalar1=-HUGE, scalar2=HUGE, op0=ALU.mult, op1=ALU.add
                )
            groups = [(bt, g) for bt in BLOCK_TILES for g in range(GROUPS_OF_TILE)]
            parts_of = {}

            def by_factor(columns):
                return columns.rearrange("p (T u v) -> p u T v", u=LANES, v=QUADS)

            def bound_blocks(parts, name):
                bounds, divisors = by_factor(parts["bound_" + name][:]), by_factor(parts["divisor_" + name][:])
                for u in range(LANES):
                    nc.scalar.activation(
                        out=bounds[:, u], in_=divisors[:, u], func=ACT.Identity, bias=alien[name][:, u : u + 1], scale=EPS
                    )

            for bt, g in groups:
                parts = {}
                for name in names:
                    for kind in ("bound_", "divisor_", "root_"):
                        parts[kind + name] = soft.tile([P, GROUP_COLS], F32, name="%s%s_%d%d" % (kind, name, bt, g))
                    nc.gpsimd.memset(parts["divisor_" + name][:], 1.0)
                    bound_blocks(parts, name)
                    parts[name] = soft.tile([P, GROUP_COLS + WIDE], F32, name="%s_%d%d" % (name, bt, g))
                    nc.gpsimd.memset(parts[name][:], 0.0)
                nc.vector.tensor_copy(
                    out=parts["a"][:, 0:GROUP_COLS].rearrange("p (T x y) -> p T x y", x=LANES, y=QUADS),
                    in_=lane_mask[:].unsqueeze(1).unsqueeze(3).to_broadcast([P, GROUP_BLOCKS, LANES, QUADS]),
                )
                parts["sums"] = banks.tile([P, BANK], F32, tag="bank", name="sums_%d%d" % (bt, g))
                parts_of[bt, g] = parts
            natural = {
                (bt, name): soft.tile([P, P], F32, name="natural_%s%d" % (name, bt)) for bt in BLOCK_TILES for name in names
            }

            def add_up_blocks(bt, g, step):
                parts = parts_of[bt, g]
                blocks, factor = (by_i[bt], parts["a"]) if step % 2 == 0 else (by_j[bt], parts["c"])
                for T in range(GROUP_BLOCKS):
                    block = GROUP_BLOCKS * g + T
                    nth = GROUP_BLOCKS * groups.index((bt, g)) + T
                    cols = slice(UNIT * T, UNIT * T + (WIDE if nth < WIDE_BLOCKS else NARROW))
                    nc.tensor.matmul(
                        parts["sums"][:, cols], blocks[:, P * block : P * (block + 1)], factor[:, cols], start=True, stop=True
                    )

            def divide_blocks(bt, g, step):
                parts = parts_of[bt, g]
                name = names[step % 2]
                divisor = parts["divisor_" + name]
                own_order = dict(u=LANES, v=QUADS)
                nc.vector.tensor_tensor(
                    out=divisor[:].rearrange("p (T u v) -> p T u v", **own_order),
                    in0=parts["sums"][:, 0:GROUP_COLS].rearrange("p (T v u) -> p T u v", **own_order),
                    in1=parts["bound_" + name][:].rearrange("p (T u v) -> p T u v", **own_order),
                    op=ALU.max,
                )

            def renew_blocks(bt, g, step):
                parts = parts_of[bt, g]
                name = names[step % 2]
                divisor, root = parts["divisor_" + name], parts["root_" + name]
                nc.scalar.activation(out=root[:], in_=divisor[:], func=ACT.Abs_reciprocal_sqrt, bias=tiny[:], scale=1.0)
                if step + 1 < STEPS:
                    nc.scalar.activation(out=parts[name][:, 0:GROUP_COLS], in_=root[:], func=ACT.Square)
                if step + 2 >= STEPS:
                    pattern = "p (u T v) -> p u T v" if name == "c" else "p (v T u) -> p u T v"
                    columns = natural[bt, name][:].rearrange(pattern, T=BLOCKS, u=LANES)
                    nc.scalar.activation(
                        out=columns[:, :, GROUP_BLOCKS * g : GROUP_BLOCKS * (g + 1), :], in_=by_factor(root[:]), func=ACT.Square
                    )

            def to_rows(bt, name):
                rows = soft.tile([P, SIDE], F32, name="rows_%s%d" % (name, bt))
                first = BANK // 2 if name == "c" else BANK // 2 + P
                sums = parts_of[bt, GROUPS_OF_TILE - 1]["sums"][:, first : first + SIDE]
                picks = pick_j if name == "c" else pick_i
                nc.tensor.matmul(sums, natural[bt, name][:], picks[:], start=True, stop=True)
                nc.vector.tensor_copy(out=rows[:], in_=sums)
                return rows

            state = {}
            for bt in (OWN_TILE, LENT_TILE):
                mine = {}
                for name in names:
                    mine[name] = soft.tile([P, SIDE], F32, name="%s%d" % (name, bt))
                    mine["bounds_" + name] = soft.tile([P, 2, SIDE], F32, name="bounds_%s%d" % (name, bt))
                    nc.vector.memset(mine["bounds_" + name][:, 1, :], EPS)
                mine["divisor"] = soft.tile([P, SIDE], F32, name="divisor%d" % bt)
                mine["root"] = soft.tile([P, SIDE], F32, name="root%d" % bt)
                mine["prod"] = soft.tile([P, DOUT], F32, name="prod%d" % bt)
                state[bt] = mine
            nc.vector.memset(state[OWN_TILE]["a"][:], 1.0)

            def multiply_own(step):
                mine = state[OWN_TILE]
                for h, bank in enumerate(own_banks):
                    rows = slice(HALF_SIDE * h, HALF_SIDE * (h + 1))
                    if step % 2 == 0:
                        out_view = mine["prod"][:].rearrange("p (j i) -> p j i", i=SIDE)[:, :, rows]
                        in_view = bank[:].rearrange("p (i j) -> p j i", j=SIDE)
                        factor = mine["a"][:, rows].unsqueeze(1).to_broadcast([P, SIDE, HALF_SIDE])
                    else:
                        out_view = mine["prod"][:].rearrange("p (i j) -> p i j", j=SIDE)[:, rows, :]
                        in_view = bank[:].rearrange("p (i j) -> p i j", j=SIDE)
                        factor = mine["c"][:].unsqueeze(1).to_broadcast([P, HALF_SIDE, SIDE])
                    nc.vector.tensor_tensor(out=out_view, in0=in_view, in1=factor, op=ALU.mult)

            def add_up_own(step):
                mine = state[OWN_TILE]
                nc.vector.tensor_reduce(
                    out=mine["bounds_" + names[step % 2]][:, 0, :],
                    in_=mine["prod"][:].rearrange("p (s t) -> p s t", t=SIDE),
                    axis=AXIS.X,
                    op=ALU.add,
                )

            def multiply_lent(step):
                mine = state[LENT_TILE]
                matrix, factor = (lent_ji, mine["a"]) if step % 2 == 0 else (lent_ij, mine["c"])
                for rows in LENT_PIECES:
                    nc.gpsimd.tensor_tensor(
                        out=mine["prod"][:].rearrange("p (s t) -> p s t", t=SIDE)[:, rows, :],
                        in0=matrix[:].rearrange("p (s t) -> p s t", t=SIDE)[:, rows, :],
                        in1=factor[:].unsqueeze(1).to_broadcast([P, rows.stop - rows.start, SIDE]),
                        op=ALU.mult,
                    )

            def add_up_lent(step, rows):
                mine = state[LENT_TILE]
                terms = (lent_ji if step == 0 else mine["prod"])[:].rearrange("p (s t) -> p s t", t=SIDE)
                nc.vector.tensor_reduce(
                    out=mine["bounds_" + names[step % 2]][:, 0, rows], in_=terms[:, rows, :], axis=AXIS.X, op=ALU.add
                )

            def renew(bt, step):
                mine = state[bt]
                name = names[step % 2]
                bounds = mine["bounds_" + name]
                nc.vector.tensor_reduce(
                    out=mine["divisor"][:], in_=bounds[:].rearrange("p plane s -> p s plane"), axis=AXIS.X, op=ALU.max
                )
                nc.scalar.activation(
                    out=mine["root"][:], in_=mine["divisor"][:], func=ACT.Abs_reciprocal_sqrt, bias=tiny[:], scale=1.0
                )
                nc.scalar.activation(out=mine[name][:], in_=mine["root"][:], func=ACT.Square)
                nc.scalar.mul(out=bounds[:, 1, :], in_=mine["divisor"][:], mul=EPS)

            def store(bt, result, rows):
                nc.sync.dma_start(
                    out=out[P * bt : P * (bt + 1), rows, :].rearrange("b i j -> b (i j)"),
                    in_=result[:, SIDE * rows.start : SIDE * rows.stop],
                )

            def finish(bt, result, a, engine, halves=(0, 1)):
                by_matrix = result[:].rearrange("p (i j) -> p i j", j=SIDE)
                for half in halves:
                    rows = slice(HALF_SIDE * half, HALF_SIDE * (half + 1))
                    engine.tensor_tensor(
                        out=by_matrix[:, rows, :],
                        in0=by_matrix[:, rows, :],
                        in1=a[:, rows].unsqueeze(2).to_broadcast([P, HALF_SIDE, SIDE]),
                        op=ALU.mult,
                    )
                    store(bt, result, rows)

            def finish_on_scalar(bt, result, a, half):
                rows = slice(HALF_SIDE * half, HALF_SIDE * (half + 1))
                for i in range(rows.start, rows.stop):
                    row = result[:, SIDE * i : SIDE * (i + 1)]
                    nc.scalar.activation(out=row, in_=row, func=ACT.Copy, scale=a[:, i : i + 1])
                store(bt, result, rows)

            results = {bt: soft.tile([P, DOUT], F32, name="result%d" % bt) for bt in BLOCK_TILES}

            def times_c(bt):
                rows_c = to_rows(bt, "c")
                for h in range(HALVES):
                    bank = flip_back(bt, h)
                    nc.vector.tensor_tensor(
                        out=results[bt][:, BANK * h : BANK * (h + 1)].rearrange("p (i j) -> p i j", j=SIDE),
                        in0=bank[:].rearrange("p (i j) -> p i j", j=SIDE),
                        in1=rows_c[:].unsqueeze(1).to_broadcast([P, HALF_SIDE, SIDE]),
                        op=ALU.mult,
                    )

            with tc.manual_schedule():
                for step in range(STEPS):
                    for bt, g in groups[:-1]:
                        add_up_blocks(bt, g, step)
                    multiply_own(step)
                    if step > 0:
                        divide_blocks(*groups[-1], step - 1)
                        renew_blocks(*groups[-1], step - 1)
                    add_up_blocks(*groups[-1], step)
                    add_up_own(step)
                    divide_blocks(*groups[0], step)
                    renew_blocks(*groups[0], step)
                    renew(OWN_TILE, step)
                    if 0 < step < STEPS - 1:
                        bound_blocks(parts_of[groups[-1]], names[(step - 1) % 2])
                    add_up_lent(step, LENT_PIECES[0])
                    divide_blocks(*groups[1], step)
                    renew_blocks(*groups[1], step)
                    add_up_lent(step, LENT_PIECES[1])
                    divide_blocks(*groups[2], step)
                    renew(LENT_TILE, step)
                    if step + 1 < STEPS:
                        multiply_lent(step + 1)
                    renew_blocks(*groups[2], step)
                    if step + 2 < STEPS:
                        for group in groups[:-1]:
                            bound_blocks(parts_of[group], names[step % 2])
                divide_blocks(*groups[-1], STEPS - 1)
                renew_blocks(*groups[-1], STEPS - 1)
                for half in range(2):
                    finish_on_scalar(OWN_TILE, state[OWN_TILE]["prod"], state[OWN_TILE]["a"], half)
                finish(LENT_TILE, state[LENT_TILE]["prod"], state[LENT_TILE]["a"], nc.gpsimd)
                for bt in BLOCK_TILES:
                    times_c(bt)
                rows_a = {bt: to_rows(bt, "a") for bt in BLOCK_TILES}
                first, last = BLOCK_TILES
                finish(first, results[first], rows_a[first], nc.vector)
                finish(last, results[last], rows_a[last], nc.vector, halves=(0,))
                finish_on_scalar(last, results[last], rows_a[last], 1)
